import numpy as np
import ml_dtypes


def mxq(x, axis, fmt="e4m3"):
    dtype, down = {"e4m3": (ml_dtypes.float8_e4m3fn, 7), "e5m2": (ml_dtypes.float8_e5m2, 14)}[fmt]
    v = np.moveaxis(np.asarray(x, np.float32).astype(ml_dtypes.bfloat16).astype(np.float64), axis, -1)
    blocks = v.reshape(v.shape[:-1] + (-1, 32))
    amax = np.abs(blocks).max(-1, keepdims=True)
    byte = np.maximum(np.where(amax > 0, np.frexp(amax)[1] - 1 + 127, 0) - down, 1)
    scale = np.exp2(byte - 127.0)
    codes = (blocks / scale).astype(np.float32).astype(dtype).astype(np.float64)
    return np.moveaxis((codes * scale).reshape(v.shape), -1, axis)


WIDE = False


def mx_kscale(k):
    if not WIDE:
        return np.ones(k)
    levels = np.array([10, -10, 5, -5, 0])
    a = np.random.permutation(np.resize(levels, k // 512 * 4)).reshape(k // 512, 4)
    idx = np.arange(k)
    return np.exp2(a[idx // 512, idx % 128 // 32])


BF16 = ml_dtypes.bfloat16


def bf(x):
    return np.asarray(x, np.float32).astype(BF16)


def f64(x):
    return np.asarray(x).astype(np.float64)


B, D, S, O = 1024, 512, 1024, 256
K1 = D + S
P = S // 2
EPS = 1e-6


def sigmoid(v):
    return 1.0 / (1.0 + np.exp(-v))


def setup_inputs():
    r = np.random.standard_normal
    s = np.concatenate([mx_kscale(D), np.ones(S)])
    t = mx_kscale(S)
    return {
        "inputs": bf(r((B, D)) * s[:D]),
        "states": bf(r((B, S))),
        "W1": bf(r((K1, S)) / np.sqrt(K1) / s[:, None] * t),
        "b1": bf(r(S) * 0.2 * t),
        "W2": bf(r((S, P)) / np.sqrt(S) / t[:, None]),
        "b2": bf(r(P) * 0.2),
        "excitatory_potential": bf(1.0 + 0.1 * r(S)),
        "inhibitory_potential": bf(-1.0 + 0.1 * r(S)),
        "capacitance": bf(1.0 + 0.1 * r(S)),
        "max_conductance": bf(1.0 + 0.1 * r((S, 2))),
        "mean_conductance_potential": bf(0.3 * r((S, 2))),
        "std_conductance": bf(1.0 + 0.2 * r((S, 2))),
        "gamma": bf(1.0 + 0.1 * r(S)),
        "beta": bf(0.1 * r(S)),
    }


def reference(inputs, states, W1, b1, W2, b2, excitatory_potential, inhibitory_potential, capacitance,
              max_conductance, mean_conductance_potential, std_conductance, gamma, beta):
    v = f64(states)
    b, s = v.shape
    intervals = np.ones((b, 1))
    cat = np.concatenate([f64(inputs), v], -1)
    h = (mxq(cat, 1, "e4m3") @ mxq(f64(W1), 0, "e4m3")) + f64(b1)
    pre = (mxq(h, 1, "e4m3") @ mxq(f64(W2), 0, "e4m3")) + f64(b2)
    memory_cell_inputs = np.stack([pre, -pre], -1).reshape(b, s)
    pairs = v.reshape(b, s // 2, 2)
    rolled = np.roll(pairs, 1, axis=-1)
    presyn = np.concatenate([pairs, rolled], -1).reshape(b, s, 2)
    g = f64(max_conductance) * sigmoid(f64(std_conductance) * (presyn - f64(mean_conductance_potential)))
    rev = np.stack([f64(excitatory_potential), f64(inhibitory_potential)], -1)
    diff = rev - v[..., None]
    states_change = (memory_cell_inputs + np.sum(g * diff, -1)) / f64(capacitance) * intervals
    x = v + states_change
    mu = np.mean(x, -1, keepdims=True)
    var = np.mean((x - mu) ** 2, -1, keepdims=True)
    return (x - mu) * (1.0 / np.sqrt(var + EPS)) * f64(gamma) + f64(beta)

@@ -1,0 +1,437 @@
+from contextlib import ExitStack
+
+import concourse.mybir as mybir
+from concourse.masks import make_identity
+
+F32 = mybir.dt.float32
+BF16 = mybir.dt.bfloat16
+U32 = mybir.dt.uint32
+U8 = mybir.dt.uint8
+FP8X4 = mybir.dt.float8_e4m3fn_x4
+ALU = mybir.AluOpType
+FUNC = mybir.ActivationFunctionType
+
+P = 128
+PACK = 4
+K_PASS = P * PACK
+BANK = 512
+
+ROWS, D_IN, CELLS = 1024, 512, 1024
+PAIRS = CELLS // 2
+K1 = D_IN + CELLS
+EPS = 1e-6
+
+ROW_TILES = ROWS // P
+HALF = ROWS // 2
+HALVES = 2
+TILES_PER_HALF = HALF // P
+PASSES_1 = K1 // K_PASS
+PASSES_2 = CELLS // K_PASS
+PAIR_BLOCKS = PAIRS // P
+N_COLS = 2 * PAIR_BLOCKS
+
+FLOPS = 2 * ROWS * K1 * CELLS + 2 * ROWS * CELLS * PAIRS
+
+
+def tile_memorylayercell_pa_kernel(
+    tc,
+    inputs,
+    states,
+    W1,
+    b1,
+    W2,
+    b2,
+    excitatory_potential,
+    inhibitory_potential,
+    capacitance,
+    max_conductance,
+    mean_conductance_potential,
+    std_conductance,
+    gamma,
+    beta,
+    out,
+):
+    nc = tc.nc
+    with ExitStack() as ctx:
+        consts = ctx.enter_context(tc.tile_pool(name="consts", bufs=1))
+        keep = ctx.enter_context(tc.tile_pool(name="keep", bufs=1))
+        terms = ctx.enter_context(tc.tile_pool(name="terms", bufs=1))
+        small = ctx.enter_context(tc.tile_pool(name="small", bufs=4))
+        psum = ctx.enter_context(tc.psum_pool(name="psum", bufs=8))
+
+        def new_bank(label):
+            return psum.tile([P, BANK], F32, name=label, tag="bank")
+
+        ident_f32 = consts.tile([P, P], F32)
+        make_identity(nc, ident_f32[:])
+        ident_bf16 = consts.tile([P, P], BF16)
+        make_identity(nc, ident_bf16[:])
+
+        vec_rows = consts.tile([P, 2 * P], BF16)
+        mat_rows = consts.tile([P, 4 * P], BF16)
+        bias_rows = consts.tile([P, P], BF16)
+        nc.vector.memset(vec_rows[:], 0.0)
+        nc.vector.memset(mat_rows[:], 0.0)
+        nc.vector.memset(bias_rows[:], 0.0)
+        for k, vec in enumerate((excitatory_potential, inhibitory_potential, capacitance)):
+            nc.scalar.dma_start(
+                out=vec_rows[4 * k : 4 * k + 4, :],
+                in_=vec.rearrange("(j c) -> j c", j=PAIR_BLOCKS),
+            )
+        for k, mat in enumerate((max_conductance, mean_conductance_potential, std_conductance)):
+            nc.scalar.dma_start(
+                out=mat_rows[4 * k : 4 * k + 4, :],
+                in_=mat.rearrange("(j c) s -> j (c s)", j=PAIR_BLOCKS),
+            )
+        nc.scalar.dma_start(out=bias_rows[0:8, :], in_=b1.rearrange("(j c) -> j c", c=P))
+        nc.scalar.dma_start(out=bias_rows[8:12, :], in_=b2.rearrange("(j c) -> j c", c=P))
+
+        with (
+            tc.tile_pool(name="natural", bufs=1) as natural,
+            tc.tile_pool(name="w_raw", bufs=3) as w_raw_pool,
+            tc.tile_pool(name="w_grouped", bufs=2) as w_grouped_pool,
+        ):
+
+            states_rows = states.rearrange("(p t) s -> p t s", t=ROW_TILES)
+            inputs_rows = inputs.rearrange("(p t) s -> p t s", t=ROW_TILES)
+            out_rows = out.rearrange("(p t) s -> p t s", t=ROW_TILES)
+            states_nat = natural.tile([P, ROW_TILES, CELLS], BF16)
+            inputs_nat = natural.tile([P, ROW_TILES, D_IN], BF16)
+
+            def load_rows(h):
+                tiles = slice(TILES_PER_HALF * h, TILES_PER_HALF * (h + 1))
+                nc.sync.dma_start(out=states_nat[:, tiles, :], in_=states_rows[:, tiles, :])
+                nc.sync.dma_start(out=inputs_nat[:, tiles, :], in_=inputs_rows[:, tiles, :])
+
+            def load_w1(g):
+                raw = w_raw_pool.tile([P, PACK, CELLS], BF16, name="w1_raw", tag="w_raw")
+                nc.sync.dma_start(
+                    out=raw[:].rearrange("q (u e) s -> q u e s", u=2),
+                    in_=W1[K_PASS * g : K_PASS * (g + 1), :].rearrange(
+                        "(u q e) s -> q u e s", u=2, e=2
+                    ),
+                )
+                return raw
+
+            load_rows(0)
+            w1_raw = [load_w1(g) for g in range(PASSES_1)]
+            load_rows(1)
+            w2_raw = w_raw_pool.tile([P, PASSES_2, PACK, PAIRS], BF16, name="w2_raw", tag="w_raw")
+            nc.sync.dma_start(
+                out=w2_raw[:], in_=W2.rearrange("(g t p) n -> p g t n", g=PASSES_2, t=PACK)
+            )
+
+            const_bank = new_bank("const_bank")
+            vec_words = vec_rows[:].bitcast(F32)
+            mat_words = mat_rows[:].bitcast(F32).rearrange("r (w e) -> r w e", e=2)
+            nc.tensor.transpose(const_bank[:, 0:P], vec_words, ident_f32[:])
+            for e in range(2):
+                nc.tensor.transpose(
+                    const_bank[:, P * (1 + e) : P * (2 + e)], mat_words[:, :, e], ident_f32[:]
+                )
+            const_words = consts.tile([P, 3 * P], F32)
+            nc.vector.tensor_copy(out=const_words[:], in_=const_bank[:, 0 : 3 * P])
+            const_bf16 = const_words[:].bitcast(BF16)
+
+            bias_bank = psum.tile([P, P], BF16, name="bias_bank", tag="bank")
+            nc.tensor.transpose(bias_bank[:], bias_rows[:], ident_bf16[:])
+            biases = consts.tile([P, 12], F32)
+            nc.vector.tensor_copy(out=biases[:], in_=bias_bank[:, 0:12])
+            b1_cols = biases[:, 0:8]
+            b2_cols = biases[:, 8:12]
+
+            vecs = consts.tile([P, 3, N_COLS], F32)
+            nc.vector.tensor_copy(
+                out=vecs[:].rearrange("p k c -> p (k c)"), in_=const_bf16[:, 0 : 3 * N_COLS]
+            )
+            mats = consts.tile([P, 3, 2, PAIR_BLOCKS, 2], F32)
+            for e in range(2):
+                first = 2 * P * (1 + e)
+                nc.vector.tensor_copy(
+                    out=mats[:, :, :, :, e],
+                    in_=const_bf16[:, first : first + 24].rearrange(
+                        "p (k j s) -> p k s j", k=3, j=PAIR_BLOCKS, s=2
+                    ),
+                )
+            reversal = vecs[:, 0:2, :]
+            max_cond = mats[:, 0, :, :, :].rearrange("p s j e -> p s (j e)")
+            mean_pot = mats[:, 1, :, :, :].rearrange("p s j e -> p s (j e)")
+            slope = mats[:, 2, :, :, :].rearrange("p s j e -> p s (j e)")
+
+            inv_cap = consts.tile([P, N_COLS], F32)
+            nc.vector.reciprocal(out=inv_cap[:], in_=vecs[:, 2, :])
+            neg_gain = consts.tile([P, 2, N_COLS], F32)
+            nc.vector.scalar_tensor_tensor(
+                out=neg_gain[:],
+                in0=max_cond,
+                scalar=-1.0,
+                in1=inv_cap[:].unsqueeze(1).to_broadcast([P, 2, N_COLS]),
+                op0=ALU.mult,
+                op1=ALU.mult,
+            )
+            shift = consts.tile([P, 2, N_COLS], F32)
+            nc.vector.scalar_tensor_tensor(
+                out=shift[:], in0=slope, scalar=-1.0, in1=mean_pot, op0=ALU.mult, op1=ALU.mult
+            )
+            sign = consts.tile([P, PAIR_BLOCKS, 2], F32)
+            nc.vector.memset(sign[:, :, 0], 1.0)
+            nc.vector.memset(sign[:, :, 1], -1.0)
+            drive_gain = consts.tile([P, N_COLS], F32)
+            nc.vector.tensor_mul(
+                out=drive_gain[:], in0=inv_cap[:], in1=sign[:].rearrange("p j e -> p (j e)")
+            )
+            drive_bias = consts.tile([P, N_COLS], F32)
+            nc.vector.tensor_mul(
+                out=drive_bias[:].rearrange("p (j e) -> p j e", e=2),
+                in0=drive_gain[:].rearrange("p (j e) -> p j e", e=2),
+                in1=b2_cols.unsqueeze(2).to_broadcast([P, PAIR_BLOCKS, 2]),
+            )
+            nc.vector.tensor_add(out=drive_bias[:], in0=drive_bias[:], in1=vecs[:, 0, :])
+            neg_half = consts.tile([P, 1], F32)
+            nc.vector.memset(neg_half[:], -0.5)
+
+            cat_grouped = keep.tile([P, PASSES_1, ROWS, PACK], BF16, align_bytes=64)
+            cat_codes = keep.tile([P, PASSES_1, ROWS], U32, align_bytes=64)
+            cat_scales = keep.tile([P, PASSES_1, ROWS], U8, align_bytes=64)
+            cat_words = cat_grouped[:].bitcast(F32)
+            inputs_words = inputs_nat[:].bitcast(F32)
+            states_words = states_nat[:].bitcast(F32)
+
+            def transpose_cat(g, t0):
+                bank = new_bank("cat_bank")
+                for u in range(2):
+                    for i in range(2):
+                        if g == 0:
+                            words = inputs_words[:, t0 + i, P * u : P * (u + 1)]
+                        else:
+                            first = 2 * P * (g - 1) + P * u
+                            words = states_words[:, t0 + i, first : first + P]
+                        nc.tensor.transpose(
+                            bank[:, P * (2 * u + i) : P * (2 * u + i + 1)], words, ident_f32[:]
+                        )
+                nc.scalar.copy(
+                    out=cat_words[:, g, P * t0 : P * (t0 + 2), :],
+                    in_=bank[:].rearrange("p (u r) -> p r u", u=2),
+                )
+
+            def quantise_cat(g, h):
+                rows = slice(HALF * h, HALF * (h + 1))
+                nc.vector.quantize_mx(
+                    out=cat_codes[:, g, rows].bitcast(FP8X4),
+                    scales=cat_scales[:, g, rows],
+                    in_=cat_grouped[:, g, rows, :].rearrange("p r t -> p (r t)"),
+                )
+
+            for h in range(HALVES):
+                for g in (1, 2, 0):
+                    for t0 in range(TILES_PER_HALF * h, TILES_PER_HALF * (h + 1), 2):
+                        transpose_cat(g, t0)
+                for g in range(PASSES_1):
+                    quantise_cat(g, h)
+
+            w1_codes = keep.tile([P, PASSES_1, CELLS], U32, align_bytes=64)
+            w1_scales = keep.tile([P, PASSES_1, CELLS], U8, align_bytes=64)
+            w2_codes = keep.tile([P, PASSES_2, PAIRS], U32, align_bytes=64)
+            w2_scales = keep.tile([P, PASSES_2, PAIRS], U8, align_bytes=64)
+
+            def regroup(dst, src):
+                nc.vector.tensor_copy(
+                    out=dst.rearrange("p (c i) t -> p c t i", i=4),
+                    in_=src.rearrange("p t (c i) -> p c t i", i=4),
+                )
+
+            for g in range(PASSES_1):
+                w1_grouped = w_grouped_pool.tile(
+                    [P, CELLS, PACK], BF16, name="w1_grouped", tag="w_grouped", align_bytes=64
+                )
+                regroup(w1_grouped[:], w1_raw[g][:])
+                nc.vector.quantize_mx(
+                    out=w1_codes[:, g, :].bitcast(FP8X4),
+                    scales=w1_scales[:, g, :],
+                    in_=w1_grouped[:].rearrange("p c t -> p (c t)"),
+                )
+            w2_grouped = w_grouped_pool.tile(
+                [P, PASSES_2, PAIRS, PACK], BF16, name="w2_grouped", tag="w_grouped", align_bytes=64
+            )
+            for g in range(PASSES_2):
+                regroup(w2_grouped[:, g, :, :], w2_raw[:, g, :, :])
+            nc.vector.quantize_mx(
+                out=w2_codes[:].rearrange("p g c -> p (g c)").bitcast(FP8X4),
+                scales=w2_scales[:].rearrange("p g c -> p (g c)"),
+                in_=w2_grouped[:].rearrange("p g c t -> p (g c t)"),
+            )
+
+        late = ctx.enter_context(tc.tile_pool(name="late", bufs=1))
+        row_pool = ctx.enter_context(tc.tile_pool(name="row_pool", bufs=2))
+        gamma_rows = late.tile([P, CELLS], BF16)
+        beta_rows = late.tile([P, CELLS], BF16)
+        nc.sync.dma_start(out=gamma_rows[:], in_=gamma.partition_broadcast(P))
+        nc.sync.dma_start(out=beta_rows[:], in_=beta.partition_broadcast(P))
+
+        h_grouped = keep.tile([P, PASSES_2, ROWS, PACK], BF16, align_bytes=64)
+        h_codes = keep.tile([P, PASSES_2, ROWS], U32, align_bytes=64)
+        h_scales = keep.tile([P, PASSES_2, ROWS], U8, align_bytes=64)
+
+        def first_product(g2, t):
+            rows = slice(P * t, P * (t + 1))
+            bank = new_bank("h_bank")
+            for t4 in range(PACK):
+                cols = slice(K_PASS * g2 + P * t4, K_PASS * g2 + P * (t4 + 1))
+                for g in range(PASSES_1):
+                    nc.tensor.matmul_mx(
+                        out=bank[:, P * t4 : P * (t4 + 1)],
+                        lhsT=w1_codes[:, g, cols].bitcast(FP8X4),
+                        lhsT_scale=w1_scales[:, g, cols],
+                        rhs=cat_codes[:, g, rows].bitcast(FP8X4),
+                        rhs_scale=cat_scales[:, g, rows],
+                        start=(g == 0),
+                        stop=(g == PASSES_1 - 1),
+                    )
+            nc.vector.tensor_tensor(
+                out=h_grouped[:, g2, rows, :],
+                in0=bank[:].rearrange("p (t r) -> p r t", t=PACK),
+                in1=b1_cols[:, PACK * g2 : PACK * (g2 + 1)].unsqueeze(1).to_broadcast([P, P, PACK]),
+                op=ALU.add,
+            )
+
+        def quantise_h(g2, h):
+            rows = slice(HALF * h, HALF * (h + 1))
+            nc.vector.quantize_mx(
+                out=h_codes[:, g2, rows].bitcast(FP8X4),
+                scales=h_scales[:, g2, rows],
+                in_=h_grouped[:, g2, rows, :].rearrange("p r t -> p (r t)"),
+            )
+
+        for h in range(HALVES):
+            for g2 in range(PASSES_2):
+                for t in range(TILES_PER_HALF * h, TILES_PER_HALF * (h + 1)):
+                    first_product(g2, t)
+                quantise_h(g2, h)
+
+        drive = {}
+
+        def second_product(h, jb):
+            rows = slice(HALF * h, HALF * (h + 1))
+            cols = slice(P * jb, P * (jb + 1))
+            bank = new_bank("pre_bank")
+            for g2 in range(PASSES_2):
+                nc.tensor.matmul_mx(
+                    out=bank[:],
+                    lhsT=w2_codes[:, g2, cols].bitcast(FP8X4),
+                    lhsT_scale=w2_scales[:, g2, cols],
+                    rhs=h_codes[:, g2, rows].bitcast(FP8X4),
+                    rhs_scale=h_scales[:, g2, rows],
+                    start=(g2 == 0),
+                    stop=(g2 == PASSES_2 - 1),
+                )
+            for e in range(2):
+                c = 2 * jb + e
+                drive[h, jb, e] = late.tile([P, HALF], F32, name="drive_%d_%d_%d" % (h, jb, e))
+                nc.scalar.activation(
+                    out=drive[h, jb, e][:],
+                    in_=bank[:],
+                    func=FUNC.Identity,
+                    scale=drive_gain[:, c : c + 1],
+                    bias=drive_bias[:, c : c + 1],
+                )
+
+        for h in range(HALVES):
+            for jb in range(PAIR_BLOCKS):
+                second_product(h, jb)
+
+        self_term = {}
+        partner_term = {}
+
+        def currents(h, jb, e):
+            rows = slice(HALF * h, HALF * (h + 1))
+            c = 2 * jb + e
+            g, u = 1 + jb // 2, jb % 2
+            v_own = cat_grouped[:, g, rows, 2 * u + e]
+            v_partner = cat_grouped[:, g, rows, 2 * u + 1 - e]
+            own = terms.tile([P, HALF], F32, name="self_%d_%d_%d" % (h, jb, e))
+            other = terms.tile([P, HALF], F32, name="partner_%d_%d_%d" % (h, jb, e))
+            for syn, (dst, v_pre, offset) in enumerate(((own, v_own, 1.0), (other, v_partner, 0.0))):
+                nc.scalar.activation(
+                    out=dst[:],
+                    in_=v_pre,
+                    func=FUNC.Sigmoid,
+                    scale=slope[:, syn, c : c + 1],
+                    bias=shift[:, syn, c : c + 1],
+                )
+                nc.scalar.activation(
+                    out=dst[:],
+                    in_=dst[:],
+                    func=FUNC.Identity,
+                    scale=neg_gain[:, syn, c : c + 1],
+                    bias=offset,
+                )
+                nc.vector.scalar_tensor_tensor(
+                    out=dst[:],
+                    in0=v_own,
+                    scalar=reversal[:, syn, c : c + 1],
+                    in1=dst[:],
+                    op0=ALU.subtract,
+                    op1=ALU.mult,
+                )
+            self_term[h, jb, e] = own
+            partner_term[h, jb, e] = other
+
+        for h in range(HALVES):
+            for jb in range(PAIR_BLOCKS):
+                for e in range(2):
+                    currents(h, jb, e)
+
+        def finish_rows(t):
+            h, lanes = t // TILES_PER_HALF, slice(P * (t % TILES_PER_HALF), P * (t % TILES_PER_HALF + 1))
+            stats = small.tile([P, 2, 6], F32, name="stats")
+            x_banks = []
+            for k in range(2):
+                bank = new_bank("x_bank")
+                for e in range(2):
+                    for jl in range(2):
+                        jb = 2 * k + jl
+                        block = slice(P * (2 * e + jl), P * (2 * e + jl + 1))
+                        parts = (self_term[h, jb, e], partner_term[h, jb, e], drive[h, jb, e])
+                        for i, part in enumerate(parts):
+                            nc.tensor.matmul(
+                                out=bank[:, block],
+                                lhsT=part[:, lanes],
+                                rhs=ident_f32[:],
+                                is_transpose=True,
+                                start=(i == 0),
+                                stop=(i == len(parts) - 1),
+                            )
+                nc.vector.bn_stats(out=stats[:, k, :], in_=bank[:])
+                x_banks.append(bank)
+            mean_var = small.tile([P, 2], F32, name="mean_var")
+            nc.vector.bn_aggr(out=mean_var[:], in_=stats[:].rearrange("p k s -> p (k s)"))
+            var_eps = small.tile([P, 1], F32, name="var_eps")
+            nc.gpsimd.tensor_scalar(
+                out=var_eps[:], in0=mean_var[:, 1:2], scalar1=1.0, scalar2=EPS, op0=ALU.mult, op1=ALU.add
+            )
+            rstd = small.tile([P, 1], F32, name="rstd")
+            nc.gpsimd.tensor_tensor(out=rstd[:], in0=var_eps[:], in1=neg_half[:], op=ALU.pow)
+            centred = row_pool.tile([P, CELLS], F32, name="centred")
+            for k in range(2):
+                cells = slice(BANK * k, BANK * (k + 1))
+                nc.vector.scalar_tensor_tensor(
+                    out=centred[:, cells].rearrange("p (q e) -> p q e", e=2),
+                    in0=x_banks[k][:].rearrange("p (e q) -> p q e", e=2),
+                    scalar=mean_var[:, 0:1],
+                    in1=gamma_rows[:, cells].rearrange("p (q e) -> p q e", e=2),
+                    op0=ALU.subtract,
+                    op1=ALU.mult,
+                )
+            result = row_pool.tile([P, CELLS], F32, name="result")
+            nc.vector.scalar_tensor_tensor(
+                out=result[:],
+                in0=centred[:],
+                scalar=rstd[:, 0:1],
+                in1=beta_rows[:],
+                op0=ALU.mult,
+                op1=ALU.add,
+            )
+            nc.sync.dma_start(out=out_rows[:, t, :], in_=result[:])
+
+        for t in range(ROW_TILES):
+            finish_rows(t)

@@ -113,8 +113,10 @@ def tile_memorylayercell_pa_kernel(
                 )
                 return raw
 
+            w1_raw = [load_w1(0)]
             load_rows(0)
-            w1_raw = [load_w1(g) for g in range(PASSES_1)]
+            w1_raw.append(load_w1(1))
+            w1_raw.append(load_w1(2))
             load_rows(1)
             w2_raw = w_raw_pool.tile([P, PASSES_2, PACK, PAIRS], BF16, name="w2_raw", tag="w_raw")
             nc.sync.dma_start(
@@ -263,6 +265,7 @@ def tile_memorylayercell_pa_kernel(
 
         late = ctx.enter_context(tc.tile_pool(name="late", bufs=1))
         row_pool = ctx.enter_context(tc.tile_pool(name="row_pool", bufs=2))
+        unused_pool = ctx.enter_context(tc.tile_pool(name="unused_pool", bufs=4))
         gamma_rows = late.tile([P, CELLS], BF16)
         beta_rows = late.tile([P, CELLS], BF16)
         nc.sync.dma_start(out=gamma_rows[:], in_=gamma.partition_broadcast(P))
@@ -350,7 +353,7 @@ def tile_memorylayercell_pa_kernel(
             v_partner = cat_grouped[:, g, rows, 2 * u + 1 - e]
             own = terms.tile([P, HALF], F32, name="self_%d_%d_%d" % (h, jb, e))
             other = terms.tile([P, HALF], F32, name="partner_%d_%d_%d" % (h, jb, e))
-            for syn, (dst, v_pre, offset) in enumerate(((own, v_own, 1.0), (other, v_partner, 0.0))):
+            for syn, (dst, v_pre) in enumerate(((own, v_own), (other, v_partner))):
                 nc.scalar.activation(
                     out=dst[:],
                     in_=v_pre,
@@ -358,13 +361,11 @@ def tile_memorylayercell_pa_kernel(
                     scale=slope[:, syn, c : c + 1],
                     bias=shift[:, syn, c : c + 1],
                 )
-                nc.scalar.activation(
-                    out=dst[:],
-                    in_=dst[:],
-                    func=FUNC.Identity,
-                    scale=neg_gain[:, syn, c : c + 1],
-                    bias=offset,
-                )
+            nc.scalar.activation(
+                out=own[:], in_=own[:], func=FUNC.Identity, scale=neg_gain[:, 0, c : c + 1], bias=1.0
+            )
+            nc.vector.tensor_scalar_mul(out=other[:], in0=other[:], scalar1=neg_gain[:, 1, c : c + 1])
+            for syn, dst in enumerate((own, other)):
                 nc.vector.scalar_tensor_tensor(
                     out=dst[:],
                     in0=v_own,
@@ -383,7 +384,7 @@ def tile_memorylayercell_pa_kernel(
 
         def finish_rows(t):
             h, lanes = t // TILES_PER_HALF, slice(P * (t % TILES_PER_HALF), P * (t % TILES_PER_HALF + 1))
-            stats = small.tile([P, 2, 6], F32, name="stats")
+            neg_mean_parts = small.tile([P, 2], F32, name="neg_mean_parts")
             x_banks = []
             for k in range(2):
                 bank = new_bank("x_bank")
@@ -401,13 +402,36 @@ def tile_memorylayercell_pa_kernel(
                                 start=(i == 0),
                                 stop=(i == len(parts) - 1),
                             )
-                nc.vector.bn_stats(out=stats[:, k, :], in_=bank[:])
+                unused = unused_pool.tile([P, BANK], BF16, name="unused")
+                nc.scalar.activation(
+                    out=unused[:],
+                    in_=bank[:],
+                    func=FUNC.Identity,
+                    scale=-1.0 / CELLS,
+                    accum_out=neg_mean_parts[:, k : k + 1],
+                )
                 x_banks.append(bank)
-            mean_var = small.tile([P, 2], F32, name="mean_var")
-            nc.vector.bn_aggr(out=mean_var[:], in_=stats[:].rearrange("p k s -> p (k s)"))
+            neg_mean = small.tile([P, 1], F32, name="neg_mean")
+            nc.gpsimd.tensor_tensor(
+                out=neg_mean[:], in0=neg_mean_parts[:, 0:1], in1=neg_mean_parts[:, 1:2], op=ALU.add
+            )
+            square_parts = small.tile([P, 2], F32, name="square_parts")
+            for k in range(2):
+                unused = unused_pool.tile([P, BANK], BF16, name="unused")
+                nc.scalar.activation(
+                    out=unused[:],
+                    in_=x_banks[k][:],
+                    func=FUNC.Square,
+                    bias=neg_mean[:, 0:1],
+                    accum_out=square_parts[:, k : k + 1],
+                )
+            squares = small.tile([P, 1], F32, name="squares")
+            nc.gpsimd.tensor_tensor(
+                out=squares[:], in0=square_parts[:, 0:1], in1=square_parts[:, 1:2], op=ALU.add
+            )
             var_eps = small.tile([P, 1], F32, name="var_eps")
             nc.gpsimd.tensor_scalar(
-                out=var_eps[:], in0=mean_var[:, 1:2], scalar1=1.0, scalar2=EPS, op0=ALU.mult, op1=ALU.add
+                out=var_eps[:], in0=squares[:], scalar1=1.0 / CELLS, scalar2=EPS, op0=ALU.mult, op1=ALU.add
             )
             rstd = small.tile([P, 1], F32, name="rstd")
             nc.gpsimd.tensor_tensor(out=rstd[:], in0=var_eps[:], in1=neg_half[:], op=ALU.pow)
@@ -417,9 +441,9 @@ def tile_memorylayercell_pa_kernel(
                 nc.vector.scalar_tensor_tensor(
                     out=centred[:, cells].rearrange("p (q e) -> p q e", e=2),
                     in0=x_banks[k][:].rearrange("p (e q) -> p q e", e=2),
-                    scalar=mean_var[:, 0:1],
+                    scalar=neg_mean[:, 0:1],
                     in1=gamma_rows[:, cells].rearrange("p (q e) -> p q e", e=2),
-                    op0=ALU.subtract,
+                    op0=ALU.add,
                     op1=ALU.mult,
                 )
             result = row_pool.tile([P, CELLS], F32, name="result")

@@ -412,8 +412,11 @@ def tile_memorylayercell_pa_kernel(
                 )
                 x_banks.append(bank)
             neg_mean = small.tile([P, 1], F32, name="neg_mean")
-            nc.gpsimd.tensor_tensor(
-                out=neg_mean[:], in0=neg_mean_parts[:, 0:1], in1=neg_mean_parts[:, 1:2], op=ALU.add
+            nc.scalar.activation(
+                out=neg_mean[:],
+                in_=neg_mean_parts[:, 0:1],
+                func=FUNC.Identity,
+                bias=neg_mean_parts[:, 1:2],
             )
             square_parts = small.tile([P, 2], F32, name="square_parts")
             for k in range(2):
@@ -425,13 +428,17 @@ def tile_memorylayercell_pa_kernel(
                     bias=neg_mean[:, 0:1],
                     accum_out=square_parts[:, k : k + 1],
                 )
-            squares = small.tile([P, 1], F32, name="squares")
-            nc.gpsimd.tensor_tensor(
-                out=squares[:], in0=square_parts[:, 0:1], in1=square_parts[:, 1:2], op=ALU.add
+            part_eps = small.tile([P, 1], F32, name="part_eps")
+            nc.scalar.activation(
+                out=part_eps[:], in_=square_parts[:, 1:2], func=FUNC.Identity, scale=1.0 / CELLS, bias=EPS
             )
             var_eps = small.tile([P, 1], F32, name="var_eps")
-            nc.gpsimd.tensor_scalar(
-                out=var_eps[:], in0=squares[:], scalar1=1.0 / CELLS, scalar2=EPS, op0=ALU.mult, op1=ALU.add
+            nc.scalar.activation(
+                out=var_eps[:],
+                in_=square_parts[:, 0:1],
+                func=FUNC.Identity,
+                scale=1.0 / CELLS,
+                bias=part_eps[:, 0:1],
             )
             rstd = small.tile([P, 1], F32, name="rstd")
             nc.gpsimd.tensor_tensor(out=rstd[:], in0=var_eps[:], in1=neg_half[:], op=ALU.pow)

@@ -56,7 +56,7 @@ def tile_memorylayercell_pa_kernel(
         consts = ctx.enter_context(tc.tile_pool(name="consts", bufs=1))
         keep = ctx.enter_context(tc.tile_pool(name="keep", bufs=1))
         terms = ctx.enter_context(tc.tile_pool(name="terms", bufs=1))
-        small = ctx.enter_context(tc.tile_pool(name="small", bufs=4))
+        small = ctx.enter_context(tc.tile_pool(name="small", bufs=8))
         psum = ctx.enter_context(tc.psum_pool(name="psum", bufs=8))
 
         def new_bank(label):
@@ -99,8 +99,12 @@ def tile_memorylayercell_pa_kernel(
             inputs_nat = natural.tile([P, ROW_TILES, D_IN], BF16)
 
             def load_rows(h):
-                tiles = slice(TILES_PER_HALF * h, TILES_PER_HALF * (h + 1))
-                nc.sync.dma_start(out=states_nat[:, tiles, :], in_=states_rows[:, tiles, :])
+                first = TILES_PER_HALF * h
+                for t0 in (first, first + 2):
+                    nc.sync.dma_start(
+                        out=states_nat[:, t0 : t0 + 2, :], in_=states_rows[:, t0 : t0 + 2, :]
+                    )
+                tiles = slice(first, first + TILES_PER_HALF)
                 nc.sync.dma_start(out=inputs_nat[:, tiles, :], in_=inputs_rows[:, tiles, :])
 
             def load_w1(g):
@@ -189,6 +193,14 @@ def tile_memorylayercell_pa_kernel(
                 in1=b2_cols.unsqueeze(2).to_broadcast([P, PAIR_BLOCKS, 2]),
             )
             nc.vector.tensor_add(out=drive_bias[:], in0=drive_bias[:], in1=vecs[:, 0, :])
+            gain_diag = consts.tile([P, N_COLS, P], F32)
+            for c in range(N_COLS):
+                nc.scalar.activation(
+                    out=gain_diag[:, c, :],
+                    in_=ident_f32[:],
+                    func=FUNC.Copy,
+                    scale=neg_gain[:, 1, c : c + 1],
+                )
             neg_half = consts.tile([P, 1], F32)
             nc.vector.memset(neg_half[:], -0.5)
 
@@ -364,7 +376,6 @@ def tile_memorylayercell_pa_kernel(
             nc.scalar.activation(
                 out=own[:], in_=own[:], func=FUNC.Identity, scale=neg_gain[:, 0, c : c + 1], bias=1.0
             )
-            nc.vector.tensor_scalar_mul(out=other[:], in0=other[:], scalar1=neg_gain[:, 1, c : c + 1])
             for syn, dst in enumerate((own, other)):
                 nc.vector.scalar_tensor_tensor(
                     out=dst[:],
@@ -384,7 +395,8 @@ def tile_memorylayercell_pa_kernel(
 
         def finish_rows(t):
             h, lanes = t // TILES_PER_HALF, slice(P * (t % TILES_PER_HALF), P * (t % TILES_PER_HALF + 1))
-            neg_mean_parts = small.tile([P, 2], F32, name="neg_mean_parts")
+            first_part = small.tile([P, 1], F32, name="first_part")
+            neg_mean = small.tile([P, 1], F32, name="neg_mean")
             x_banks = []
             for k in range(2):
                 bank = new_bank("x_bank")
@@ -392,31 +404,46 @@ def tile_memorylayercell_pa_kernel(
                     for jl in range(2):
                         jb = 2 * k + jl
                         block = slice(P * (2 * e + jl), P * (2 * e + jl + 1))
-                        parts = (self_term[h, jb, e], partner_term[h, jb, e], drive[h, jb, e])
-                        for i, part in enumerate(parts):
-                            nc.tensor.matmul(
-                                out=bank[:, block],
-                                lhsT=part[:, lanes],
-                                rhs=ident_f32[:],
-                                is_transpose=True,
-                                start=(i == 0),
-                                stop=(i == len(parts) - 1),
-                            )
-                unused = unused_pool.tile([P, BANK], BF16, name="unused")
-                nc.scalar.activation(
-                    out=unused[:],
-                    in_=bank[:],
-                    func=FUNC.Identity,
-                    scale=-1.0 / CELLS,
-                    accum_out=neg_mean_parts[:, k : k + 1],
-                )
+                        nc.tensor.matmul(
+                            out=bank[:, block],
+                            lhsT=self_term[h, jb, e][:, lanes],
+                            rhs=ident_f32[:],
+                            is_transpose=True,
+                            start=True,
+                            stop=False,
+                        )
+                        nc.tensor.matmul(
+                            out=bank[:, block],
+                            lhsT=partner_term[h, jb, e][:, lanes],
+                            rhs=gain_diag[:, 2 * jb + e, :],
+                            start=False,
+                            stop=False,
+                        )
+                        nc.tensor.matmul(
+                            out=bank[:, block],
+                            lhsT=drive[h, jb, e][:, lanes],
+                            rhs=ident_f32[:],
+                            is_transpose=True,
+                            start=False,
+                            stop=True,
+                        )
                 x_banks.append(bank)
-            neg_mean = small.tile([P, 1], F32, name="neg_mean")
+            unused = unused_pool.tile([P, BANK], BF16, name="unused")
             nc.scalar.activation(
-                out=neg_mean[:],
-                in_=neg_mean_parts[:, 0:1],
+                out=unused[:],
+                in_=x_banks[0][:],
                 func=FUNC.Identity,
-                bias=neg_mean_parts[:, 1:2],
+                scale=-1.0 / (CELLS * BANK),
+                accum_out=first_part[:],
+            )
+            unused = unused_pool.tile([P, BANK], BF16, name="unused")
+            nc.scalar.activation(
+                out=unused[:],
+                in_=x_banks[1][:],
+                func=FUNC.Identity,
+                scale=-1.0 / CELLS,
+                bias=first_part[:, 0:1],
+                accum_out=neg_mean[:],
             )
             square_parts = small.tile([P, 2], F32, name="square_parts")
             for k in range(2):

@@ -15,6 +15,7 @@ P = 128
 PACK = 4
 K_PASS = P * PACK
 BANK = 512
+PSUM_BANKS = 8
 
 ROWS, D_IN, CELLS = 1024, 512, 1024
 PAIRS = CELLS // 2
@@ -23,12 +24,12 @@ EPS = 1e-6
 
 ROW_TILES = ROWS // P
 HALF = ROWS // 2
-HALVES = 2
 TILES_PER_HALF = HALF // P
 PASSES_1 = K1 // K_PASS
 PASSES_2 = CELLS // K_PASS
 PAIR_BLOCKS = PAIRS // P
 N_COLS = 2 * PAIR_BLOCKS
+SYNAPSES = 2
 
 FLOPS = 2 * ROWS * K1 * CELLS + 2 * ROWS * CELLS * PAIRS
 
@@ -53,14 +54,25 @@ def tile_memorylayercell_pa_kernel(
 ):
     nc = tc.nc
     with ExitStack() as ctx:
+        ctx.enter_context(tc.manual_schedule())
         consts = ctx.enter_context(tc.tile_pool(name="consts", bufs=1))
         keep = ctx.enter_context(tc.tile_pool(name="keep", bufs=1))
         terms = ctx.enter_context(tc.tile_pool(name="terms", bufs=1))
-        small = ctx.enter_context(tc.tile_pool(name="small", bufs=8))
-        psum = ctx.enter_context(tc.psum_pool(name="psum", bufs=8))
+        small = ctx.enter_context(tc.tile_pool(name="small", bufs=ROW_TILES))
+        psum = ctx.enter_context(tc.psum_pool(name="psum", bufs=PSUM_BANKS))
 
         def new_bank(label):
             return psum.tile([P, BANK], F32, name=label, tag="bank")
+
+        states_rows = states.rearrange("(p t) s -> p t s", t=ROW_TILES)
+        inputs_rows = inputs.rearrange("(p t) s -> p t s", t=ROW_TILES)
+        out_rows = out.rearrange("(p t) s -> p t s", t=ROW_TILES)
+
+        def tiles_of(h):
+            return slice(TILES_PER_HALF * h, TILES_PER_HALF * (h + 1))
+
+        def rows_of(h):
+            return slice(HALF * h, HALF * (h + 1))
 
         ident_f32 = consts.tile([P, P], F32)
         make_identity(nc, ident_f32[:])
@@ -73,39 +85,25 @@ def tile_memorylayercell_pa_kernel(
         nc.vector.memset(vec_rows[:], 0.0)
         nc.vector.memset(mat_rows[:], 0.0)
         nc.vector.memset(bias_rows[:], 0.0)
-        for k, vec in enumerate((excitatory_potential, inhibitory_potential, capacitance)):
-            nc.scalar.dma_start(
-                out=vec_rows[4 * k : 4 * k + 4, :],
-                in_=vec.rearrange("(j c) -> j c", j=PAIR_BLOCKS),
-            )
-        for k, mat in enumerate((max_conductance, mean_conductance_potential, std_conductance)):
-            nc.scalar.dma_start(
-                out=mat_rows[4 * k : 4 * k + 4, :],
-                in_=mat.rearrange("(j c) s -> j (c s)", j=PAIR_BLOCKS),
-            )
-        nc.scalar.dma_start(out=bias_rows[0:8, :], in_=b1.rearrange("(j c) -> j c", c=P))
-        nc.scalar.dma_start(out=bias_rows[8:12, :], in_=b2.rearrange("(j c) -> j c", c=P))
+        neg_half = consts.tile([P, 1], F32)
+        nc.vector.memset(neg_half[:], -0.5)
+        gain_offset = consts.tile([P, SYNAPSES], F32)
+        nc.vector.memset(gain_offset[:, 0:1], 1.0)
+        nc.vector.memset(gain_offset[:, 1:2], 0.0)
+        sign = consts.tile([P, PAIR_BLOCKS, 2], F32)
+        nc.vector.memset(sign[:, :, 0], 1.0)
+        nc.vector.memset(sign[:, :, 1], -1.0)
+
+        states_nat = keep.tile([P, ROW_TILES, CELLS], BF16)
+        states_words = states_nat[:].bitcast(F32)
 
         with (
-            tc.tile_pool(name="natural", bufs=1) as natural,
+            tc.tile_pool(name="early", bufs=1) as early,
             tc.tile_pool(name="w_raw", bufs=3) as w_raw_pool,
             tc.tile_pool(name="w_grouped", bufs=2) as w_grouped_pool,
         ):
-
-            states_rows = states.rearrange("(p t) s -> p t s", t=ROW_TILES)
-            inputs_rows = inputs.rearrange("(p t) s -> p t s", t=ROW_TILES)
-            out_rows = out.rearrange("(p t) s -> p t s", t=ROW_TILES)
-            states_nat = natural.tile([P, ROW_TILES, CELLS], BF16)
-            inputs_nat = natural.tile([P, ROW_TILES, D_IN], BF16)
-
-            def load_rows(h):
-                first = TILES_PER_HALF * h
-                for t0 in (first, first + 2):
-                    nc.sync.dma_start(
-                        out=states_nat[:, t0 : t0 + 2, :], in_=states_rows[:, t0 : t0 + 2, :]
-                    )
-                tiles = slice(first, first + TILES_PER_HALF)
-                nc.sync.dma_start(out=inputs_nat[:, tiles, :], in_=inputs_rows[:, tiles, :])
+            inputs_nat = early.tile([P, ROW_TILES, D_IN], BF16)
+            inputs_words = inputs_nat[:].bitcast(F32)
 
             def load_w1(g):
                 raw = w_raw_pool.tile([P, PACK, CELLS], BF16, name="w1_raw", tag="w_raw")
@@ -118,341 +116,372 @@ def tile_memorylayercell_pa_kernel(
                 return raw
 
             w1_raw = [load_w1(0)]
-            load_rows(0)
+            nc.sync.dma_start(out=states_nat[:, tiles_of(0), :], in_=states_rows[:, tiles_of(0), :])
+            for k, vec in enumerate((excitatory_potential, inhibitory_potential, capacitance)):
+                nc.scalar.dma_start(
+                    out=vec_rows[4 * k : 4 * k + 4, :],
+                    in_=vec.rearrange("(j c) -> j c", j=PAIR_BLOCKS),
+                )
+            for k, mat in enumerate((max_conductance, mean_conductance_potential, std_conductance)):
+                nc.scalar.dma_start(
+                    out=mat_rows[4 * k : 4 * k + 4, :],
+                    in_=mat.rearrange("(j c) s -> j (c s)", j=PAIR_BLOCKS),
+                )
+            warm = consts.tile([P, 1], F32)
+            nc.scalar.activation(out=warm[:], in_=neg_half[:], func=FUNC.Sigmoid)
             w1_raw.append(load_w1(1))
             w1_raw.append(load_w1(2))
-            load_rows(1)
+            nc.scalar.dma_start(out=bias_rows[0:8, :], in_=b1.rearrange("(j c) -> j c", c=P))
+            nc.scalar.dma_start(out=bias_rows[8:12, :], in_=b2.rearrange("(j c) -> j c", c=P))
+            nc.sync.dma_start(out=inputs_nat[:, tiles_of(0), :], in_=inputs_rows[:, tiles_of(0), :])
             w2_raw = w_raw_pool.tile([P, PASSES_2, PACK, PAIRS], BF16, name="w2_raw", tag="w_raw")
             nc.sync.dma_start(
                 out=w2_raw[:], in_=W2.rearrange("(g t p) n -> p g t n", g=PASSES_2, t=PACK)
             )
+            nc.sync.dma_start(out=states_nat[:, tiles_of(1), :], in_=states_rows[:, tiles_of(1), :])
+            nc.sync.dma_start(out=inputs_nat[:, tiles_of(1), :], in_=inputs_rows[:, tiles_of(1), :])
 
             const_bank = new_bank("const_bank")
-            vec_words = vec_rows[:].bitcast(F32)
-            mat_words = mat_rows[:].bitcast(F32).rearrange("r (w e) -> r w e", e=2)
-            nc.tensor.transpose(const_bank[:, 0:P], vec_words, ident_f32[:])
-            for e in range(2):
-                nc.tensor.transpose(
-                    const_bank[:, P * (1 + e) : P * (2 + e)], mat_words[:, :, e], ident_f32[:]
-                )
-            const_words = consts.tile([P, 3 * P], F32)
-            nc.vector.tensor_copy(out=const_words[:], in_=const_bank[:, 0 : 3 * P])
-            const_bf16 = const_words[:].bitcast(BF16)
-
             bias_bank = psum.tile([P, P], BF16, name="bias_bank", tag="bank")
-            nc.tensor.transpose(bias_bank[:], bias_rows[:], ident_bf16[:])
-            biases = consts.tile([P, 12], F32)
-            nc.vector.tensor_copy(out=biases[:], in_=bias_bank[:, 0:12])
-            b1_cols = biases[:, 0:8]
-            b2_cols = biases[:, 8:12]
-
+            const_words = consts.tile([P, 3 * P], F32)
+            const_bf16 = const_words[:].bitcast(BF16)
             vecs = consts.tile([P, 3, N_COLS], F32)
-            nc.vector.tensor_copy(
-                out=vecs[:].rearrange("p k c -> p (k c)"), in_=const_bf16[:, 0 : 3 * N_COLS]
-            )
-            mats = consts.tile([P, 3, 2, PAIR_BLOCKS, 2], F32)
-            for e in range(2):
-                first = 2 * P * (1 + e)
-                nc.vector.tensor_copy(
-                    out=mats[:, :, :, :, e],
-                    in_=const_bf16[:, first : first + 24].rearrange(
-                        "p (k j s) -> p k s j", k=3, j=PAIR_BLOCKS, s=2
-                    ),
-                )
+            mats = consts.tile([P, 3, SYNAPSES, PAIR_BLOCKS, 2], F32)
             reversal = vecs[:, 0:2, :]
             max_cond = mats[:, 0, :, :, :].rearrange("p s j e -> p s (j e)")
             mean_pot = mats[:, 1, :, :, :].rearrange("p s j e -> p s (j e)")
             slope = mats[:, 2, :, :, :].rearrange("p s j e -> p s (j e)")
-
+            shift = consts.tile([P, SYNAPSES, N_COLS], F32)
             inv_cap = consts.tile([P, N_COLS], F32)
-            nc.vector.reciprocal(out=inv_cap[:], in_=vecs[:, 2, :])
-            neg_gain = consts.tile([P, 2, N_COLS], F32)
-            nc.vector.scalar_tensor_tensor(
-                out=neg_gain[:],
-                in0=max_cond,
-                scalar=-1.0,
-                in1=inv_cap[:].unsqueeze(1).to_broadcast([P, 2, N_COLS]),
-                op0=ALU.mult,
-                op1=ALU.mult,
-            )
-            shift = consts.tile([P, 2, N_COLS], F32)
-            nc.vector.scalar_tensor_tensor(
-                out=shift[:], in0=slope, scalar=-1.0, in1=mean_pot, op0=ALU.mult, op1=ALU.mult
-            )
-            sign = consts.tile([P, PAIR_BLOCKS, 2], F32)
-            nc.vector.memset(sign[:, :, 0], 1.0)
-            nc.vector.memset(sign[:, :, 1], -1.0)
+            neg_gain = consts.tile([P, SYNAPSES, N_COLS], F32)
             drive_gain = consts.tile([P, N_COLS], F32)
-            nc.vector.tensor_mul(
-                out=drive_gain[:], in0=inv_cap[:], in1=sign[:].rearrange("p j e -> p (j e)")
-            )
             drive_bias = consts.tile([P, N_COLS], F32)
-            nc.vector.tensor_mul(
-                out=drive_bias[:].rearrange("p (j e) -> p j e", e=2),
-                in0=drive_gain[:].rearrange("p (j e) -> p j e", e=2),
-                in1=b2_cols.unsqueeze(2).to_broadcast([P, PAIR_BLOCKS, 2]),
-            )
-            nc.vector.tensor_add(out=drive_bias[:], in0=drive_bias[:], in1=vecs[:, 0, :])
-            gain_diag = consts.tile([P, N_COLS, P], F32)
-            for c in range(N_COLS):
-                nc.scalar.activation(
-                    out=gain_diag[:, c, :],
-                    in_=ident_f32[:],
-                    func=FUNC.Copy,
-                    scale=neg_gain[:, 1, c : c + 1],
-                )
-            neg_half = consts.tile([P, 1], F32)
-            nc.vector.memset(neg_half[:], -0.5)
+            biases = consts.tile([P, 12], F32)
+            b1_cols = biases[:, 0:8]
+            b2_cols = biases[:, 8:12]
 
-            cat_grouped = keep.tile([P, PASSES_1, ROWS, PACK], BF16, align_bytes=64)
+            def transpose_cell_constants():
+                vec_words = vec_rows[:].bitcast(F32)
+                mat_words = mat_rows[:].bitcast(F32).rearrange("r (w e) -> r w e", e=2)
+                nc.tensor.transpose(const_bank[:, 0:P], vec_words, ident_f32[:])
+                for e in range(2):
+                    nc.tensor.transpose(
+                        const_bank[:, P * (1 + e) : P * (2 + e)], mat_words[:, :, e], ident_f32[:]
+                    )
+
+            def combine_cell_constants():
+                nc.vector.tensor_copy(out=const_words[:], in_=const_bank[:, 0 : 3 * P])
+                nc.vector.tensor_copy(
+                    out=vecs[:].rearrange("p k c -> p (k c)"), in_=const_bf16[:, 0 : 3 * N_COLS]
+                )
+                for e in range(2):
+                    first = 2 * P * (1 + e)
+                    nc.vector.tensor_copy(
+                        out=mats[:, :, :, :, e],
+                        in_=const_bf16[:, first : first + 24].rearrange(
+                            "p (k j s) -> p k s j", k=3, j=PAIR_BLOCKS, s=SYNAPSES
+                        ),
+                    )
+                nc.vector.scalar_tensor_tensor(
+                    out=shift[:], in0=slope, scalar=-1.0, in1=mean_pot, op0=ALU.mult, op1=ALU.mult
+                )
+                nc.vector.reciprocal(out=inv_cap[:], in_=vecs[:, 2, :])
+                nc.vector.scalar_tensor_tensor(
+                    out=neg_gain[:],
+                    in0=max_cond,
+                    scalar=-1.0,
+                    in1=inv_cap[:].unsqueeze(1).to_broadcast([P, SYNAPSES, N_COLS]),
+                    op0=ALU.mult,
+                    op1=ALU.mult,
+                )
+                nc.vector.tensor_mul(
+                    out=drive_gain[:], in0=inv_cap[:], in1=sign[:].rearrange("p j e -> p (j e)")
+                )
+
+            def transpose_biases():
+                nc.tensor.transpose(bias_bank[:], bias_rows[:], ident_bf16[:])
+
+            def combine_biases():
+                nc.vector.tensor_copy(out=biases[:], in_=bias_bank[:, 0:12])
+                nc.vector.tensor_mul(
+                    out=drive_bias[:].rearrange("p (j e) -> p j e", e=2),
+                    in0=drive_gain[:].rearrange("p (j e) -> p j e", e=2),
+                    in1=b2_cols.unsqueeze(2).to_broadcast([P, PAIR_BLOCKS, 2]),
+                )
+                nc.vector.tensor_add(out=drive_bias[:], in0=drive_bias[:], in1=vecs[:, 0, :])
+
+            cat_grouped = [
+                pool.tile([P, ROWS, PACK], BF16, name="cat_grouped_%d" % g, align_bytes=64)
+                for g, pool in enumerate((early, keep, keep))
+            ]
             cat_codes = keep.tile([P, PASSES_1, ROWS], U32, align_bytes=64)
             cat_scales = keep.tile([P, PASSES_1, ROWS], U8, align_bytes=64)
-            cat_words = cat_grouped[:].bitcast(F32)
-            inputs_words = inputs_nat[:].bitcast(F32)
-            states_words = states_nat[:].bitcast(F32)
 
-            def transpose_cat(g, t0):
-                bank = new_bank("cat_bank")
-                for u in range(2):
-                    for i in range(2):
-                        if g == 0:
-                            words = inputs_words[:, t0 + i, P * u : P * (u + 1)]
-                        else:
-                            first = 2 * P * (g - 1) + P * u
-                            words = states_words[:, t0 + i, first : first + P]
-                        nc.tensor.transpose(
-                            bank[:, P * (2 * u + i) : P * (2 * u + i + 1)], words, ident_f32[:]
-                        )
-                nc.scalar.copy(
-                    out=cat_words[:, g, P * t0 : P * (t0 + 2), :],
-                    in_=bank[:].rearrange("p (u r) -> p r u", u=2),
-                )
+            def transpose_cat(g, h):
+                for t0 in range(TILES_PER_HALF * h, TILES_PER_HALF * (h + 1), 2):
+                    bank = new_bank("cat_bank")
+                    for u in range(2):
+                        for i in range(2):
+                            if g == 0:
+                                words = inputs_words[:, t0 + i, P * u : P * (u + 1)]
+                            else:
+                                first = 2 * P * (g - 1) + P * u
+                                words = states_words[:, t0 + i, first : first + P]
+                            nc.tensor.transpose(
+                                bank[:, P * (2 * u + i) : P * (2 * u + i + 1)], words, ident_f32[:]
+                            )
+                    nc.scalar.copy(
+                        out=cat_grouped[g][:].bitcast(F32)[:, P * t0 : P * (t0 + 2), :],
+                        in_=bank[:].rearrange("p (u r) -> p r u", u=2),
+                    )
 
             def quantise_cat(g, h):
-                rows = slice(HALF * h, HALF * (h + 1))
                 nc.vector.quantize_mx(
-                    out=cat_codes[:, g, rows].bitcast(FP8X4),
-                    scales=cat_scales[:, g, rows],
-                    in_=cat_grouped[:, g, rows, :].rearrange("p r t -> p (r t)"),
+                    out=cat_codes[:, g, rows_of(h)].bitcast(FP8X4),
+                    scales=cat_scales[:, g, rows_of(h)],
+                    in_=cat_grouped[g][:, rows_of(h), :].rearrange("p r t -> p (r t)"),
                 )
-
-            for h in range(HALVES):
-                for g in (1, 2, 0):
-                    for t0 in range(TILES_PER_HALF * h, TILES_PER_HALF * (h + 1), 2):
-                        transpose_cat(g, t0)
-                for g in range(PASSES_1):
-                    quantise_cat(g, h)
 
             w1_codes = keep.tile([P, PASSES_1, CELLS], U32, align_bytes=64)
             w1_scales = keep.tile([P, PASSES_1, CELLS], U8, align_bytes=64)
             w2_codes = keep.tile([P, PASSES_2, PAIRS], U32, align_bytes=64)
             w2_scales = keep.tile([P, PASSES_2, PAIRS], U8, align_bytes=64)
 
-            def regroup(dst, src):
-                nc.vector.tensor_copy(
-                    out=dst.rearrange("p (c i) t -> p c t i", i=4),
-                    in_=src.rearrange("p t (c i) -> p c t i", i=4),
+            def prepare_weights(raw_parts, code_parts, scale_parts):
+                grouped = w_grouped_pool.tile(
+                    [P, 2, BANK, PACK], BF16, name="w_grouped", tag="w_grouped", align_bytes=64
+                )
+                for i, raw in enumerate(raw_parts):
+                    nc.vector.tensor_copy(
+                        out=grouped[:, i, :, :].rearrange("p (c i) t -> p c t i", i=4),
+                        in_=raw.rearrange("p t (c i) -> p c t i", i=4),
+                    )
+                for i, (codes, scales) in enumerate(zip(code_parts, scale_parts)):
+                    nc.vector.quantize_mx(
+                        out=codes.bitcast(FP8X4),
+                        scales=scales,
+                        in_=grouped[:, i, :, :].rearrange("p c t -> p (c t)"),
+                    )
+
+            def prepare_w1(g):
+                parts = (slice(0, BANK), slice(BANK, 2 * BANK))
+                prepare_weights(
+                    [w1_raw[g][:, :, cols] for cols in parts],
+                    [w1_codes[:, g, cols] for cols in parts],
+                    [w1_scales[:, g, cols] for cols in parts],
                 )
 
-            for g in range(PASSES_1):
-                w1_grouped = w_grouped_pool.tile(
-                    [P, CELLS, PACK], BF16, name="w1_grouped", tag="w_grouped", align_bytes=64
+            def prepare_w2():
+                prepare_weights(
+                    [w2_raw[:, g, :, :] for g in range(PASSES_2)],
+                    [w2_codes[:, g, :] for g in range(PASSES_2)],
+                    [w2_scales[:, g, :] for g in range(PASSES_2)],
                 )
-                regroup(w1_grouped[:], w1_raw[g][:])
+
+            term = {}
+
+            def gates(h, jb):
+                g, u = 1 + jb // 2, jb % 2
+                for e in range(2):
+                    c = 2 * jb + e
+                    for syn in range(SYNAPSES):
+                        v_pre = cat_grouped[g][:, rows_of(h), 2 * u + (e + syn) % 2]
+                        gate = terms.tile([P, HALF], F32, name="term_%d_%d_%d_%d" % (h, jb, e, syn))
+                        nc.scalar.activation(
+                            out=gate[:],
+                            in_=v_pre,
+                            func=FUNC.Sigmoid,
+                            scale=slope[:, syn, c : c + 1],
+                            bias=shift[:, syn, c : c + 1],
+                        )
+                        nc.gpsimd.tensor_scalar(
+                            out=gate[:],
+                            in0=gate[:],
+                            scalar1=neg_gain[:, syn, c : c + 1],
+                            scalar2=gain_offset[:, syn : syn + 1],
+                            op0=ALU.mult,
+                            op1=ALU.add,
+                        )
+                        term[h, jb, e, syn] = gate
+
+            h_grouped = keep.tile([P, PASSES_2, ROWS, PACK], BF16, align_bytes=64)
+            h_codes = keep.tile([P, PASSES_2, ROWS], U32, align_bytes=64)
+            h_scales = keep.tile([P, PASSES_2, ROWS], U8, align_bytes=64)
+
+            def first_product(g2, t):
+                rows = slice(P * t, P * (t + 1))
+                bank = new_bank("h_bank")
+                for t4 in range(PACK):
+                    cols = slice(K_PASS * g2 + P * t4, K_PASS * g2 + P * (t4 + 1))
+                    for g in range(PASSES_1):
+                        nc.tensor.matmul_mx(
+                            out=bank[:, P * t4 : P * (t4 + 1)],
+                            lhsT=w1_codes[:, g, cols].bitcast(FP8X4),
+                            lhsT_scale=w1_scales[:, g, cols],
+                            rhs=cat_codes[:, g, rows].bitcast(FP8X4),
+                            rhs_scale=cat_scales[:, g, rows],
+                            start=(g == 0),
+                            stop=(g == PASSES_1 - 1),
+                        )
+                nc.vector.tensor_tensor(
+                    out=h_grouped[:, g2, rows, :],
+                    in0=bank[:].rearrange("p (t r) -> p r t", t=PACK),
+                    in1=b1_cols[:, PACK * g2 : PACK * (g2 + 1)]
+                    .unsqueeze(1)
+                    .to_broadcast([P, P, PACK]),
+                    op=ALU.add,
+                )
+
+            def quantise_h(g2, h):
                 nc.vector.quantize_mx(
-                    out=w1_codes[:, g, :].bitcast(FP8X4),
-                    scales=w1_scales[:, g, :],
-                    in_=w1_grouped[:].rearrange("p c t -> p (c t)"),
+                    out=h_codes[:, g2, rows_of(h)].bitcast(FP8X4),
+                    scales=h_scales[:, g2, rows_of(h)],
+                    in_=h_grouped[:, g2, rows_of(h), :].rearrange("p r t -> p (r t)"),
                 )
-            w2_grouped = w_grouped_pool.tile(
-                [P, PASSES_2, PAIRS, PACK], BF16, name="w2_grouped", tag="w_grouped", align_bytes=64
-            )
-            for g in range(PASSES_2):
-                regroup(w2_grouped[:, g, :, :], w2_raw[:, g, :, :])
-            nc.vector.quantize_mx(
-                out=w2_codes[:].rearrange("p g c -> p (g c)").bitcast(FP8X4),
-                scales=w2_scales[:].rearrange("p g c -> p (g c)"),
-                in_=w2_grouped[:].rearrange("p g c t -> p (g c t)"),
-            )
+
+            transpose_cat(1, 0)
+            transpose_cell_constants()
+            transpose_cat(2, 0)
+            prepare_w1(0)
+            combine_cell_constants()
+            gates(0, 0)
+            gates(0, 1)
+            quantise_cat(1, 0)
+            transpose_cat(0, 0)
+            transpose_biases()
+            gates(0, 2)
+            gates(0, 3)
+            prepare_w1(1)
+            quantise_cat(2, 0)
+            prepare_w1(2)
+            quantise_cat(0, 0)
+            combine_biases()
+            prepare_w2()
+
+            h_banks = [(g2, t) for g2 in range(PASSES_2) for t in range(TILES_PER_HALF)]
+            banks_ahead = PSUM_BANKS - 2 * PASSES_1
+            for g2, t in h_banks[:banks_ahead]:
+                first_product(g2, t)
+            for g in (1, 2, 0):
+                transpose_cat(g, 1)
+            for g in (1, 2, 0):
+                quantise_cat(g, 1)
 
         late = ctx.enter_context(tc.tile_pool(name="late", bufs=1))
-        row_pool = ctx.enter_context(tc.tile_pool(name="row_pool", bufs=2))
+        row_pool = ctx.enter_context(tc.tile_pool(name="row_pool", bufs=6))
         unused_pool = ctx.enter_context(tc.tile_pool(name="unused_pool", bufs=4))
         gamma_rows = late.tile([P, CELLS], BF16)
         beta_rows = late.tile([P, CELLS], BF16)
         nc.sync.dma_start(out=gamma_rows[:], in_=gamma.partition_broadcast(P))
         nc.sync.dma_start(out=beta_rows[:], in_=beta.partition_broadcast(P))
 
-        h_grouped = keep.tile([P, PASSES_2, ROWS, PACK], BF16, align_bytes=64)
-        h_codes = keep.tile([P, PASSES_2, ROWS], U32, align_bytes=64)
-        h_scales = keep.tile([P, PASSES_2, ROWS], U8, align_bytes=64)
-
-        def first_product(g2, t):
-            rows = slice(P * t, P * (t + 1))
-            bank = new_bank("h_bank")
-            for t4 in range(PACK):
-                cols = slice(K_PASS * g2 + P * t4, K_PASS * g2 + P * (t4 + 1))
-                for g in range(PASSES_1):
-                    nc.tensor.matmul_mx(
-                        out=bank[:, P * t4 : P * (t4 + 1)],
-                        lhsT=w1_codes[:, g, cols].bitcast(FP8X4),
-                        lhsT_scale=w1_scales[:, g, cols],
-                        rhs=cat_codes[:, g, rows].bitcast(FP8X4),
-                        rhs_scale=cat_scales[:, g, rows],
-                        start=(g == 0),
-                        stop=(g == PASSES_1 - 1),
-                    )
-            nc.vector.tensor_tensor(
-                out=h_grouped[:, g2, rows, :],
-                in0=bank[:].rearrange("p (t r) -> p r t", t=PACK),
-                in1=b1_cols[:, PACK * g2 : PACK * (g2 + 1)].unsqueeze(1).to_broadcast([P, P, PACK]),
-                op=ALU.add,
-            )
-
-        def quantise_h(g2, h):
-            rows = slice(HALF * h, HALF * (h + 1))
-            nc.vector.quantize_mx(
-                out=h_codes[:, g2, rows].bitcast(FP8X4),
-                scales=h_scales[:, g2, rows],
-                in_=h_grouped[:, g2, rows, :].rearrange("p r t -> p (r t)"),
-            )
-
-        for h in range(HALVES):
-            for g2 in range(PASSES_2):
-                for t in range(TILES_PER_HALF * h, TILES_PER_HALF * (h + 1)):
-                    first_product(g2, t)
-                quantise_h(g2, h)
-
         drive = {}
 
-        def second_product(h, jb):
-            rows = slice(HALF * h, HALF * (h + 1))
-            cols = slice(P * jb, P * (jb + 1))
-            bank = new_bank("pre_bank")
-            for g2 in range(PASSES_2):
-                nc.tensor.matmul_mx(
-                    out=bank[:],
-                    lhsT=w2_codes[:, g2, cols].bitcast(FP8X4),
-                    lhsT_scale=w2_scales[:, g2, cols],
-                    rhs=h_codes[:, g2, rows].bitcast(FP8X4),
-                    rhs_scale=h_scales[:, g2, rows],
-                    start=(g2 == 0),
-                    stop=(g2 == PASSES_2 - 1),
-                )
-            for e in range(2):
-                c = 2 * jb + e
-                drive[h, jb, e] = late.tile([P, HALF], F32, name="drive_%d_%d_%d" % (h, jb, e))
-                nc.scalar.activation(
-                    out=drive[h, jb, e][:],
-                    in_=bank[:],
-                    func=FUNC.Identity,
-                    scale=drive_gain[:, c : c + 1],
-                    bias=drive_bias[:, c : c + 1],
-                )
-
-        for h in range(HALVES):
+        def second_product(h):
             for jb in range(PAIR_BLOCKS):
-                second_product(h, jb)
+                cols = slice(P * jb, P * (jb + 1))
+                bank = new_bank("pre_bank")
+                for g2 in range(PASSES_2):
+                    nc.tensor.matmul_mx(
+                        out=bank[:],
+                        lhsT=w2_codes[:, g2, cols].bitcast(FP8X4),
+                        lhsT_scale=w2_scales[:, g2, cols],
+                        rhs=h_codes[:, g2, rows_of(h)].bitcast(FP8X4),
+                        rhs_scale=h_scales[:, g2, rows_of(h)],
+                        start=(g2 == 0),
+                        stop=(g2 == PASSES_2 - 1),
+                    )
+                for e in range(2):
+                    c = 2 * jb + e
+                    drive[h, jb, e] = late.tile([P, HALF], F32, name="drive_%d_%d_%d" % (h, jb, e))
+                    nc.scalar.activation(
+                        out=drive[h, jb, e][:],
+                        in_=bank[:],
+                        func=FUNC.Identity,
+                        scale=drive_gain[:, c : c + 1],
+                        bias=drive_bias[:, c : c + 1],
+                    )
 
-        self_term = {}
-        partner_term = {}
+        v_halves = {}
 
-        def currents(h, jb, e):
-            rows = slice(HALF * h, HALF * (h + 1))
-            c = 2 * jb + e
-            g, u = 1 + jb // 2, jb % 2
-            v_own = cat_grouped[:, g, rows, 2 * u + e]
-            v_partner = cat_grouped[:, g, rows, 2 * u + 1 - e]
-            own = terms.tile([P, HALF], F32, name="self_%d_%d_%d" % (h, jb, e))
-            other = terms.tile([P, HALF], F32, name="partner_%d_%d_%d" % (h, jb, e))
-            for syn, (dst, v_pre) in enumerate(((own, v_own), (other, v_partner))):
-                nc.scalar.activation(
-                    out=dst[:],
-                    in_=v_pre,
-                    func=FUNC.Sigmoid,
-                    scale=slope[:, syn, c : c + 1],
-                    bias=shift[:, syn, c : c + 1],
+        def potentials(h, jb):
+            bank = new_bank("v_bank")
+            for i in range(TILES_PER_HALF):
+                nc.tensor.transpose(
+                    bank[:, P * i : P * (i + 1)],
+                    states_words[:, TILES_PER_HALF * h + i, P * jb : P * (jb + 1)],
+                    ident_f32[:],
                 )
-            nc.scalar.activation(
-                out=own[:], in_=own[:], func=FUNC.Identity, scale=neg_gain[:, 0, c : c + 1], bias=1.0
-            )
-            for syn, dst in enumerate((own, other)):
+            v_halves[h, jb] = bank[:].bitcast(BF16).rearrange("p (r e) -> p r e", e=2)
+
+        def products(h, jb, e):
+            c = 2 * jb + e
+            for syn in range(SYNAPSES):
                 nc.vector.scalar_tensor_tensor(
-                    out=dst[:],
-                    in0=v_own,
+                    out=term[h, jb, e, syn][:],
+                    in0=v_halves[h, jb][:, :, e],
                     scalar=reversal[:, syn, c : c + 1],
-                    in1=dst[:],
+                    in1=term[h, jb, e, syn][:],
                     op0=ALU.subtract,
                     op1=ALU.mult,
                 )
-            self_term[h, jb, e] = own
-            partner_term[h, jb, e] = other
 
-        for h in range(HALVES):
-            for jb in range(PAIR_BLOCKS):
-                for e in range(2):
-                    currents(h, jb, e)
+        def currents(h, jb):
+            potentials(h, jb)
+            for e in range(2):
+                products(h, jb, e)
 
-        def finish_rows(t):
+        x_banks = {}
+        neg_mean = {}
+        rstd = {}
+        row_tile = {}
+
+        def gather_rows(t):
             h, lanes = t // TILES_PER_HALF, slice(P * (t % TILES_PER_HALF), P * (t % TILES_PER_HALF + 1))
-            first_part = small.tile([P, 1], F32, name="first_part")
-            neg_mean = small.tile([P, 1], F32, name="neg_mean")
-            x_banks = []
             for k in range(2):
                 bank = new_bank("x_bank")
                 for e in range(2):
                     for jl in range(2):
                         jb = 2 * k + jl
                         block = slice(P * (2 * e + jl), P * (2 * e + jl + 1))
-                        nc.tensor.matmul(
-                            out=bank[:, block],
-                            lhsT=self_term[h, jb, e][:, lanes],
-                            rhs=ident_f32[:],
-                            is_transpose=True,
-                            start=True,
-                            stop=False,
-                        )
-                        nc.tensor.matmul(
-                            out=bank[:, block],
-                            lhsT=partner_term[h, jb, e][:, lanes],
-                            rhs=gain_diag[:, 2 * jb + e, :],
-                            start=False,
-                            stop=False,
-                        )
-                        nc.tensor.matmul(
-                            out=bank[:, block],
-                            lhsT=drive[h, jb, e][:, lanes],
-                            rhs=ident_f32[:],
-                            is_transpose=True,
-                            start=False,
-                            stop=True,
-                        )
-                x_banks.append(bank)
-            unused = unused_pool.tile([P, BANK], BF16, name="unused")
+                        parts = (term[h, jb, e, 0], term[h, jb, e, 1], drive[h, jb, e])
+                        for i, part in enumerate(parts):
+                            nc.tensor.matmul(
+                                out=bank[:, block],
+                                lhsT=part[:, lanes],
+                                rhs=ident_f32[:],
+                                is_transpose=True,
+                                start=(i == 0),
+                                stop=(i == len(parts) - 1),
+                            )
+                x_banks[t, k] = bank
+
+        def statistics(t):
+            neg_mean_parts = small.tile([P, 2], F32, name="neg_mean_parts")
+            for k in range(2):
+                unused = unused_pool.tile([P, BANK], BF16, name="unused")
+                nc.scalar.activation(
+                    out=unused[:],
+                    in_=x_banks[t, k][:],
+                    func=FUNC.Identity,
+                    scale=-1.0 / CELLS,
+                    accum_out=neg_mean_parts[:, k : k + 1],
+                )
+            neg_mean[t] = small.tile([P, 1], F32, name="neg_mean")
             nc.scalar.activation(
-                out=unused[:],
-                in_=x_banks[0][:],
+                out=neg_mean[t][:],
+                in_=neg_mean_parts[:, 0:1],
                 func=FUNC.Identity,
-                scale=-1.0 / (CELLS * BANK),
-                accum_out=first_part[:],
-            )
-            unused = unused_pool.tile([P, BANK], BF16, name="unused")
-            nc.scalar.activation(
-                out=unused[:],
-                in_=x_banks[1][:],
-                func=FUNC.Identity,
-                scale=-1.0 / CELLS,
-                bias=first_part[:, 0:1],
-                accum_out=neg_mean[:],
+                bias=neg_mean_parts[:, 1:2],
             )
             square_parts = small.tile([P, 2], F32, name="square_parts")
             for k in range(2):
                 unused = unused_pool.tile([P, BANK], BF16, name="unused")
                 nc.scalar.activation(
                     out=unused[:],
-                    in_=x_banks[k][:],
+                    in_=x_banks[t, k][:],
                     func=FUNC.Square,
-                    bias=neg_mean[:, 0:1],
+                    bias=neg_mean[t][:, 0:1],
                     accum_out=square_parts[:, k : k + 1],
                 )
             part_eps = small.tile([P, 1], F32, name="part_eps")
@@ -467,29 +496,66 @@ def tile_memorylayercell_pa_kernel(
                 scale=1.0 / CELLS,
                 bias=part_eps[:, 0:1],
             )
-            rstd = small.tile([P, 1], F32, name="rstd")
-            nc.gpsimd.tensor_tensor(out=rstd[:], in0=var_eps[:], in1=neg_half[:], op=ALU.pow)
-            centred = row_pool.tile([P, CELLS], F32, name="centred")
+            rstd[t] = small.tile([P, 1], F32, name="rstd")
+            nc.gpsimd.tensor_tensor(out=rstd[t][:], in0=var_eps[:], in1=neg_half[:], op=ALU.pow)
+
+        def centre(t):
+            row_tile[t] = row_pool.tile([P, CELLS], F32, name="row_tile")
             for k in range(2):
                 cells = slice(BANK * k, BANK * (k + 1))
                 nc.vector.scalar_tensor_tensor(
-                    out=centred[:, cells].rearrange("p (q e) -> p q e", e=2),
-                    in0=x_banks[k][:].rearrange("p (e q) -> p q e", e=2),
-                    scalar=neg_mean[:, 0:1],
+                    out=row_tile[t][:, cells].rearrange("p (q e) -> p q e", e=2),
+                    in0=x_banks[t, k][:].rearrange("p (e q) -> p q e", e=2),
+                    scalar=neg_mean[t][:, 0:1],
                     in1=gamma_rows[:, cells].rearrange("p (q e) -> p q e", e=2),
                     op0=ALU.add,
                     op1=ALU.mult,
                 )
-            result = row_pool.tile([P, CELLS], F32, name="result")
+
+        def scale_and_store(t):
             nc.vector.scalar_tensor_tensor(
-                out=result[:],
-                in0=centred[:],
-                scalar=rstd[:, 0:1],
+                out=row_tile[t][:],
+                in0=row_tile[t][:],
+                scalar=rstd[t][:, 0:1],
                 in1=beta_rows[:],
                 op0=ALU.mult,
                 op1=ALU.add,
             )
-            nc.sync.dma_start(out=out_rows[:, t, :], in_=result[:])
+            nc.sync.dma_start(out=out_rows[:, t, :], in_=row_tile[t][:])
 
-        for t in range(ROW_TILES):
-            finish_rows(t)
+        def normalise(t):
+            gather_rows(t)
+            statistics(t)
+            centre(t)
+
+        for g2, t in h_banks[banks_ahead:]:
+            first_product(g2, t)
+        for g2 in range(PASSES_2):
+            quantise_h(g2, 0)
+        for jb in range(PAIR_BLOCKS):
+            gates(1, jb)
+
+        for g2 in range(PASSES_2):
+            potentials(0, g2)
+            for e in range(2):
+                first_product(g2, TILES_PER_HALF + 2 * e)
+                first_product(g2, TILES_PER_HALF + 2 * e + 1)
+                products(0, g2, e)
+        second_product(0)
+        for g2 in range(PASSES_2):
+            quantise_h(g2, 1)
+        for jb in range(PASSES_2, PAIR_BLOCKS):
+            currents(0, jb)
+        second_product(1)
+
+        currents(1, 0)
+        for t in range(TILES_PER_HALF):
+            if t + 1 < PAIR_BLOCKS:
+                currents(1, t + 1)
+            normalise(t)
+
+        for t in range(TILES_PER_HALF):
+            scale_and_store(t)
+        for t in range(TILES_PER_HALF, ROW_TILES):
+            normalise(t)
+            scale_and_store(t)

from contextlib import ExitStack

import concourse.mybir as mybir
from concourse.masks import make_identity

F32 = mybir.dt.float32
BF16 = mybir.dt.bfloat16
U32 = mybir.dt.uint32
U8 = mybir.dt.uint8
FP8X4 = mybir.dt.float8_e4m3fn_x4
ALU = mybir.AluOpType
FUNC = mybir.ActivationFunctionType

P = 128
PACK = 4
K_PASS = P * PACK
BANK = 512
PSUM_BANKS = 8

ROWS, D_IN, CELLS = 1024, 512, 1024
PAIRS = CELLS // 2
K1 = D_IN + CELLS
EPS = 1e-6

ROW_TILES = ROWS // P
HALF = ROWS // 2
TILES_PER_HALF = HALF // P
PASSES_1 = K1 // K_PASS
PASSES_2 = CELLS // K_PASS
PAIR_BLOCKS = PAIRS // P
N_COLS = 2 * PAIR_BLOCKS
SYNAPSES = 2

FLOPS = 2 * ROWS * K1 * CELLS + 2 * ROWS * CELLS * PAIRS


def tile_memorylayercell_pa_kernel(
    tc,
    inputs,
    states,
    W1,
    b1,
    W2,
    b2,
    excitatory_potential,
    inhibitory_potential,
    capacitance,
    max_conductance,
    mean_conductance_potential,
    std_conductance,
    gamma,
    beta,
    out,
):
    nc = tc.nc
    with ExitStack() as ctx:
        ctx.enter_context(tc.manual_schedule())
        consts = ctx.enter_context(tc.tile_pool(name="consts", bufs=1))
        keep = ctx.enter_context(tc.tile_pool(name="keep", bufs=1))
        terms = ctx.enter_context(tc.tile_pool(name="terms", bufs=1))
        small = ctx.enter_context(tc.tile_pool(name="small", bufs=ROW_TILES))
        psum = ctx.enter_context(tc.psum_pool(name="psum", bufs=PSUM_BANKS))

        def new_bank(label):
            return psum.tile([P, BANK], F32, name=label, tag="bank")

        states_rows = states.rearrange("(p t) s -> p t s", t=ROW_TILES)
        inputs_rows = inputs.rearrange("(p t) s -> p t s", t=ROW_TILES)
        out_rows = out.rearrange("(p t) s -> p t s", t=ROW_TILES)

        def tiles_of(h):
            return slice(TILES_PER_HALF * h, TILES_PER_HALF * (h + 1))

        def rows_of(h):
            return slice(HALF * h, HALF * (h + 1))

        ident_f32 = consts.tile([P, P], F32)
        make_identity(nc, ident_f32[:])
        ident_bf16 = consts.tile([P, P], BF16)
        make_identity(nc, ident_bf16[:])

        vec_rows = consts.tile([P, 2 * P], BF16)
        mat_rows = consts.tile([P, 4 * P], BF16)
        bias_rows = consts.tile([P, P], BF16)
        nc.vector.memset(vec_rows[:], 0.0)
        nc.vector.memset(mat_rows[:], 0.0)
        nc.vector.memset(bias_rows[:], 0.0)
        neg_half = consts.tile([P, 1], F32)
        nc.vector.memset(neg_half[:], -0.5)
        gain_offset = consts.tile([P, SYNAPSES], F32)
        nc.vector.memset(gain_offset[:, 0:1], 1.0)
        nc.vector.memset(gain_offset[:, 1:2], 0.0)
        sign = consts.tile([P, PAIR_BLOCKS, 2], F32)
        nc.vector.memset(sign[:, :, 0], 1.0)
        nc.vector.memset(sign[:, :, 1], -1.0)

        states_nat = keep.tile([P, ROW_TILES, CELLS], BF16)
        states_words = states_nat[:].bitcast(F32)

        with (
            tc.tile_pool(name="early", bufs=1) as early,
            tc.tile_pool(name="w_raw", bufs=3) as w_raw_pool,
            tc.tile_pool(name="w_grouped", bufs=2) as w_grouped_pool,
        ):
            inputs_nat = early.tile([P, ROW_TILES, D_IN], BF16)
            inputs_words = inputs_nat[:].bitcast(F32)

            def load_w1(g):
                raw = w_raw_pool.tile([P, PACK, CELLS], BF16, name="w1_raw", tag="w_raw")
                nc.sync.dma_start(
                    out=raw[:].rearrange("q (u e) s -> q u e s", u=2),
                    in_=W1[K_PASS * g : K_PASS * (g + 1), :].rearrange(
                        "(u q e) s -> q u e s", u=2, e=2
                    ),
                )
                return raw

            w1_raw = [load_w1(0)]
            nc.sync.dma_start(out=states_nat[:, tiles_of(0), :], in_=states_rows[:, tiles_of(0), :])
            for k, vec in enumerate((excitatory_potential, inhibitory_potential, capacitance)):
                nc.scalar.dma_start(
                    out=vec_rows[4 * k : 4 * k + 4, :],
                    in_=vec.rearrange("(j c) -> j c", j=PAIR_BLOCKS),
                )
            for k, mat in enumerate((max_conductance, mean_conductance_potential, std_conductance)):
                nc.scalar.dma_start(
                    out=mat_rows[4 * k : 4 * k + 4, :],
                    in_=mat.rearrange("(j c) s -> j (c s)", j=PAIR_BLOCKS),
                )
            warm = consts.tile([P, 1], F32)
            nc.scalar.activation(out=warm[:], in_=neg_half[:], func=FUNC.Sigmoid)
            w1_raw.append(load_w1(1))
            w1_raw.append(load_w1(2))
            nc.scalar.dma_start(out=bias_rows[0:8, :], in_=b1.rearrange("(j c) -> j c", c=P))
            nc.scalar.dma_start(out=bias_rows[8:12, :], in_=b2.rearrange("(j c) -> j c", c=P))
            nc.sync.dma_start(out=inputs_nat[:, tiles_of(0), :], in_=inputs_rows[:, tiles_of(0), :])
            w2_raw = w_raw_pool.tile([P, PASSES_2, PACK, PAIRS], BF16, name="w2_raw", tag="w_raw")
            nc.sync.dma_start(
                out=w2_raw[:], in_=W2.rearrange("(g t p) n -> p g t n", g=PASSES_2, t=PACK)
            )
            nc.sync.dma_start(out=states_nat[:, tiles_of(1), :], in_=states_rows[:, tiles_of(1), :])
            nc.sync.dma_start(out=inputs_nat[:, tiles_of(1), :], in_=inputs_rows[:, tiles_of(1), :])

            const_bank = new_bank("const_bank")
            bias_bank = psum.tile([P, P], BF16, name="bias_bank", tag="bank")
            const_words = consts.tile([P, 3 * P], F32)
            const_bf16 = const_words[:].bitcast(BF16)
            vecs = consts.tile([P, 3, N_COLS], F32)
            mats = consts.tile([P, 3, SYNAPSES, PAIR_BLOCKS, 2], F32)
            reversal = vecs[:, 0:2, :]
            max_cond = mats[:, 0, :, :, :].rearrange("p s j e -> p s (j e)")
            mean_pot = mats[:, 1, :, :, :].rearrange("p s j e -> p s (j e)")
            slope = mats[:, 2, :, :, :].rearrange("p s j e -> p s (j e)")
            shift = consts.tile([P, SYNAPSES, N_COLS], F32)
            inv_cap = consts.tile([P, N_COLS], F32)
            neg_gain = consts.tile([P, SYNAPSES, N_COLS], F32)
            drive_gain = consts.tile([P, N_COLS], F32)
            drive_bias = consts.tile([P, N_COLS], F32)
            biases = consts.tile([P, 12], F32)
            b1_cols = biases[:, 0:8]
            b2_cols = biases[:, 8:12]

            def transpose_cell_constants():
                vec_words = vec_rows[:].bitcast(F32)
                mat_words = mat_rows[:].bitcast(F32).rearrange("r (w e) -> r w e", e=2)
                nc.tensor.transpose(const_bank[:, 0:P], vec_words, ident_f32[:])
                for e in range(2):
                    nc.tensor.transpose(
                        const_bank[:, P * (1 + e) : P * (2 + e)], mat_words[:, :, e], ident_f32[:]
                    )

            def combine_cell_constants():
                nc.vector.tensor_copy(out=const_words[:], in_=const_bank[:, 0 : 3 * P])
                nc.vector.tensor_copy(
                    out=vecs[:].rearrange("p k c -> p (k c)"), in_=const_bf16[:, 0 : 3 * N_COLS]
                )
                for e in range(2):
                    first = 2 * P * (1 + e)
                    nc.vector.tensor_copy(
                        out=mats[:, :, :, :, e],
                        in_=const_bf16[:, first : first + 24].rearrange(
                            "p (k j s) -> p k s j", k=3, j=PAIR_BLOCKS, s=SYNAPSES
                        ),
                    )
                nc.vector.scalar_tensor_tensor(
                    out=shift[:], in0=slope, scalar=-1.0, in1=mean_pot, op0=ALU.mult, op1=ALU.mult
                )
                nc.vector.reciprocal(out=inv_cap[:], in_=vecs[:, 2, :])
                nc.vector.scalar_tensor_tensor(
                    out=neg_gain[:],
                    in0=max_cond,
                    scalar=-1.0,
                    in1=inv_cap[:].unsqueeze(1).to_broadcast([P, SYNAPSES, N_COLS]),
                    op0=ALU.mult,
                    op1=ALU.mult,
                )
                nc.vector.tensor_mul(
                    out=drive_gain[:], in0=inv_cap[:], in1=sign[:].rearrange("p j e -> p (j e)")
                )

            def transpose_biases():
                nc.tensor.transpose(bias_bank[:], bias_rows[:], ident_bf16[:])

            def combine_biases():
                nc.vector.tensor_copy(out=biases[:], in_=bias_bank[:, 0:12])
                nc.vector.tensor_mul(
                    out=drive_bias[:].rearrange("p (j e) -> p j e", e=2),
                    in0=drive_gain[:].rearrange("p (j e) -> p j e", e=2),
                    in1=b2_cols.unsqueeze(2).to_broadcast([P, PAIR_BLOCKS, 2]),
                )
                nc.vector.tensor_add(out=drive_bias[:], in0=drive_bias[:], in1=vecs[:, 0, :])

            cat_grouped = [
                pool.tile([P, ROWS, PACK], BF16, name="cat_grouped_%d" % g, align_bytes=64)
                for g, pool in enumerate((early, keep, keep))
            ]
            cat_codes = keep.tile([P, PASSES_1, ROWS], U32, align_bytes=64)
            cat_scales = keep.tile([P, PASSES_1, ROWS], U8, align_bytes=64)

            def transpose_cat(g, h):
                for t0 in range(TILES_PER_HALF * h, TILES_PER_HALF * (h + 1), 2):
                    bank = new_bank("cat_bank")
                    for u in range(2):
                        for i in range(2):
                            if g == 0:
                                words = inputs_words[:, t0 + i, P * u : P * (u + 1)]
                            else:
                                first = 2 * P * (g - 1) + P * u
                                words = states_words[:, t0 + i, first : first + P]
                            nc.tensor.transpose(
                                bank[:, P * (2 * u + i) : P * (2 * u + i + 1)], words, ident_f32[:]
                            )
                    nc.scalar.copy(
                        out=cat_grouped[g][:].bitcast(F32)[:, P * t0 : P * (t0 + 2), :],
                        in_=bank[:].rearrange("p (u r) -> p r u", u=2),
                    )

            def quantise_cat(g, h):
                nc.vector.quantize_mx(
                    out=cat_codes[:, g, rows_of(h)].bitcast(FP8X4),
                    scales=cat_scales[:, g, rows_of(h)],
                    in_=cat_grouped[g][:, rows_of(h), :].rearrange("p r t -> p (r t)"),
                )

            w1_codes = keep.tile([P, PASSES_1, CELLS], U32, align_bytes=64)
            w1_scales = keep.tile([P, PASSES_1, CELLS], U8, align_bytes=64)
            w2_codes = keep.tile([P, PASSES_2, PAIRS], U32, align_bytes=64)
            w2_scales = keep.tile([P, PASSES_2, PAIRS], U8, align_bytes=64)

            def prepare_weights(raw_parts, code_parts, scale_parts):
                grouped = w_grouped_pool.tile(
                    [P, 2, BANK, PACK], BF16, name="w_grouped", tag="w_grouped", align_bytes=64
                )
                for i, raw in enumerate(raw_parts):
                    nc.vector.tensor_copy(
                        out=grouped[:, i, :, :].rearrange("p (c i) t -> p c t i", i=4),
                        in_=raw.rearrange("p t (c i) -> p c t i", i=4),
                    )
                for i, (codes, scales) in enumerate(zip(code_parts, scale_parts)):
                    nc.vector.quantize_mx(
                        out=codes.bitcast(FP8X4),
                        scales=scales,
                        in_=grouped[:, i, :, :].rearrange("p c t -> p (c t)"),
                    )

            def prepare_w1(g):
                parts = (slice(0, BANK), slice(BANK, 2 * BANK))
                prepare_weights(
                    [w1_raw[g][:, :, cols] for cols in parts],
                    [w1_codes[:, g, cols] for cols in parts],
                    [w1_scales[:, g, cols] for cols in parts],
                )

            def prepare_w2():
                prepare_weights(
                    [w2_raw[:, g, :, :] for g in range(PASSES_2)],
                    [w2_codes[:, g, :] for g in range(PASSES_2)],
                    [w2_scales[:, g, :] for g in range(PASSES_2)],
                )

            term = {}

            def gates(h, jb):
                g, u = 1 + jb // 2, jb % 2
                for e in range(2):
                    c = 2 * jb + e
                    for syn in range(SYNAPSES):
                        v_pre = cat_grouped[g][:, rows_of(h), 2 * u + (e + syn) % 2]
                        gate = terms.tile([P, HALF], F32, name="term_%d_%d_%d_%d" % (h, jb, e, syn))
                        nc.scalar.activation(
                            out=gate[:],
                            in_=v_pre,
                            func=FUNC.Sigmoid,
                            scale=slope[:, syn, c : c + 1],
                            bias=shift[:, syn, c : c + 1],
                        )
                        nc.gpsimd.tensor_scalar(
                            out=gate[:],
                            in0=gate[:],
                            scalar1=neg_gain[:, syn, c : c + 1],
                            scalar2=gain_offset[:, syn : syn + 1],
                            op0=ALU.mult,
                            op1=ALU.add,
                        )
                        term[h, jb, e, syn] = gate

            h_grouped = keep.tile([P, PASSES_2, ROWS, PACK], BF16, align_bytes=64)
            h_codes = keep.tile([P, PASSES_2, ROWS], U32, align_bytes=64)
            h_scales = keep.tile([P, PASSES_2, ROWS], U8, align_bytes=64)

            def first_product(g2, t):
                rows = slice(P * t, P * (t + 1))
                bank = new_bank("h_bank")
                for t4 in range(PACK):
                    cols = slice(K_PASS * g2 + P * t4, K_PASS * g2 + P * (t4 + 1))
                    for g in range(PASSES_1):
                        nc.tensor.matmul_mx(
                            out=bank[:, P * t4 : P * (t4 + 1)],
                            lhsT=w1_codes[:, g, cols].bitcast(FP8X4),
                            lhsT_scale=w1_scales[:, g, cols],
                            rhs=cat_codes[:, g, rows].bitcast(FP8X4),
                            rhs_scale=cat_scales[:, g, rows],
                            start=(g == 0),
                            stop=(g == PASSES_1 - 1),
                        )
                nc.vector.tensor_tensor(
                    out=h_grouped[:, g2, rows, :],
                    in0=bank[:].rearrange("p (t r) -> p r t", t=PACK),
                    in1=b1_cols[:, PACK * g2 : PACK * (g2 + 1)]
                    .unsqueeze(1)
                    .to_broadcast([P, P, PACK]),
                    op=ALU.add,
                )

            def quantise_h(g2, h):
                nc.vector.quantize_mx(
                    out=h_codes[:, g2, rows_of(h)].bitcast(FP8X4),
                    scales=h_scales[:, g2, rows_of(h)],
                    in_=h_grouped[:, g2, rows_of(h), :].rearrange("p r t -> p (r t)"),
                )

            transpose_cat(1, 0)
            transpose_cell_constants()
            transpose_cat(2, 0)
            prepare_w1(0)
            combine_cell_constants()
            gates(0, 0)
            gates(0, 1)
            quantise_cat(1, 0)
            transpose_cat(0, 0)
            transpose_biases()
            gates(0, 2)
            gates(0, 3)
            prepare_w1(1)
            quantise_cat(2, 0)
            prepare_w1(2)
            quantise_cat(0, 0)
            combine_biases()
            prepare_w2()

            h_banks = [(g2, t) for g2 in range(PASSES_2) for t in range(TILES_PER_HALF)]
            banks_ahead = PSUM_BANKS - 2 * PASSES_1
            for g2, t in h_banks[:banks_ahead]:
                first_product(g2, t)
            for g in (1, 2, 0):
                transpose_cat(g, 1)
            for g in (1, 2, 0):
                quantise_cat(g, 1)

        late = ctx.enter_context(tc.tile_pool(name="late", bufs=1))
        row_pool = ctx.enter_context(tc.tile_pool(name="row_pool", bufs=6))
        unused_pool = ctx.enter_context(tc.tile_pool(name="unused_pool", bufs=4))
        gamma_rows = late.tile([P, CELLS], BF16)
        beta_rows = late.tile([P, CELLS], BF16)
        nc.sync.dma_start(out=gamma_rows[:], in_=gamma.partition_broadcast(P))
        nc.sync.dma_start(out=beta_rows[:], in_=beta.partition_broadcast(P))

        drive = {}

        def second_product(h):
            for jb in range(PAIR_BLOCKS):
                cols = slice(P * jb, P * (jb + 1))
                bank = new_bank("pre_bank")
                for g2 in range(PASSES_2):
                    nc.tensor.matmul_mx(
                        out=bank[:],
                        lhsT=w2_codes[:, g2, cols].bitcast(FP8X4),
                        lhsT_scale=w2_scales[:, g2, cols],
                        rhs=h_codes[:, g2, rows_of(h)].bitcast(FP8X4),
                        rhs_scale=h_scales[:, g2, rows_of(h)],
                        start=(g2 == 0),
                        stop=(g2 == PASSES_2 - 1),
                    )
                for e in range(2):
                    c = 2 * jb + e
                    drive[h, jb, e] = late.tile([P, HALF], F32, name="drive_%d_%d_%d" % (h, jb, e))
                    nc.scalar.activation(
                        out=drive[h, jb, e][:],
                        in_=bank[:],
                        func=FUNC.Identity,
                        scale=drive_gain[:, c : c + 1],
                        bias=drive_bias[:, c : c + 1],
                    )

        v_halves = {}

        def potentials(h, jb):
            bank = new_bank("v_bank")
            for i in range(TILES_PER_HALF):
                nc.tensor.transpose(
                    bank[:, P * i : P * (i + 1)],
                    states_words[:, TILES_PER_HALF * h + i, P * jb : P * (jb + 1)],
                    ident_f32[:],
                )
            v_halves[h, jb] = bank[:].bitcast(BF16).rearrange("p (r e) -> p r e", e=2)

        def products(h, jb, e):
            c = 2 * jb + e
            for syn in range(SYNAPSES):
                nc.vector.scalar_tensor_tensor(
                    out=term[h, jb, e, syn][:],
                    in0=v_halves[h, jb][:, :, e],
                    scalar=reversal[:, syn, c : c + 1],
                    in1=term[h, jb, e, syn][:],
                    op0=ALU.subtract,
                    op1=ALU.mult,
                )

        def currents(h, jb):
            potentials(h, jb)
            for e in range(2):
                products(h, jb, e)

        x_banks = {}
        neg_mean = {}
        rstd = {}
        row_tile = {}

        def gather_rows(t):
            h, lanes = t // TILES_PER_HALF, slice(P * (t % TILES_PER_HALF), P * (t % TILES_PER_HALF + 1))
            for k in range(2):
                bank = new_bank("x_bank")
                for e in range(2):
                    for jl in range(2):
                        jb = 2 * k + jl
                        block = slice(P * (2 * e + jl), P * (2 * e + jl + 1))
                        parts = (term[h, jb, e, 0], term[h, jb, e, 1], drive[h, jb, e])
                        for i, part in enumerate(parts):
                            nc.tensor.matmul(
                                out=bank[:, block],
                                lhsT=part[:, lanes],
                                rhs=ident_f32[:],
                                is_transpose=True,
                                start=(i == 0),
                                stop=(i == len(parts) - 1),
                            )
                x_banks[t, k] = bank

        def statistics(t):
            neg_mean_parts = small.tile([P, 2], F32, name="neg_mean_parts")
            for k in range(2):
                unused = unused_pool.tile([P, BANK], BF16, name="unused")
                nc.scalar.activation(
                    out=unused[:],
                    in_=x_banks[t, k][:],
                    func=FUNC.Identity,
                    scale=-1.0 / CELLS,
                    accum_out=neg_mean_parts[:, k : k + 1],
                )
            neg_mean[t] = small.tile([P, 1], F32, name="neg_mean")
            nc.scalar.activation(
                out=neg_mean[t][:],
                in_=neg_mean_parts[:, 0:1],
                func=FUNC.Identity,
                bias=neg_mean_parts[:, 1:2],
            )
            square_parts = small.tile([P, 2], F32, name="square_parts")
            for k in range(2):
                unused = unused_pool.tile([P, BANK], BF16, name="unused")
                nc.scalar.activation(
                    out=unused[:],
                    in_=x_banks[t, k][:],
                    func=FUNC.Square,
                    bias=neg_mean[t][:, 0:1],
                    accum_out=square_parts[:, k : k + 1],
                )
            part_eps = small.tile([P, 1], F32, name="part_eps")
            nc.scalar.activation(
                out=part_eps[:], in_=square_parts[:, 1:2], func=FUNC.Identity, scale=1.0 / CELLS, bias=EPS
            )
            var_eps = small.tile([P, 1], F32, name="var_eps")
            nc.scalar.activation(
                out=var_eps[:],
                in_=square_parts[:, 0:1],
                func=FUNC.Identity,
                scale=1.0 / CELLS,
                bias=part_eps[:, 0:1],
            )
            rstd[t] = small.tile([P, 1], F32, name="rstd")
            nc.gpsimd.tensor_tensor(out=rstd[t][:], in0=var_eps[:], in1=neg_half[:], op=ALU.pow)

        def centre(t):
            row_tile[t] = row_pool.tile([P, CELLS], F32, name="row_tile")
            for k in range(2):
                cells = slice(BANK * k, BANK * (k + 1))
                nc.vector.scalar_tensor_tensor(
                    out=row_tile[t][:, cells].rearrange("p (q e) -> p q e", e=2),
                    in0=x_banks[t, k][:].rearrange("p (e q) -> p q e", e=2),
                    scalar=neg_mean[t][:, 0:1],
                    in1=gamma_rows[:, cells].rearrange("p (q e) -> p q e", e=2),
                    op0=ALU.add,
                    op1=ALU.mult,
                )

        def scale_and_store(t):
            nc.vector.scalar_tensor_tensor(
                out=row_tile[t][:],
                in0=row_tile[t][:],
                scalar=rstd[t][:, 0:1],
                in1=beta_rows[:],
                op0=ALU.mult,
                op1=ALU.add,
            )
            nc.sync.dma_start(out=out_rows[:, t, :], in_=row_tile[t][:])

        def normalise(t):
            gather_rows(t)
            statistics(t)
            centre(t)

        for g2, t in h_banks[banks_ahead:]:
            first_product(g2, t)
        for g2 in range(PASSES_2):
            quantise_h(g2, 0)
        for jb in range(PAIR_BLOCKS):
            gates(1, jb)

        for g2 in range(PASSES_2):
            potentials(0, g2)
            for e in range(2):
                first_product(g2, TILES_PER_HALF + 2 * e)
                first_product(g2, TILES_PER_HALF + 2 * e + 1)
                products(0, g2, e)
        second_product(0)
        for g2 in range(PASSES_2):
            quantise_h(g2, 1)
        for jb in range(PASSES_2, PAIR_BLOCKS):
            currents(0, jb)
        second_product(1)

        currents(1, 0)
        for t in range(TILES_PER_HALF):
            if t + 1 < PAIR_BLOCKS:
                currents(1, t + 1)
            normalise(t)

        for t in range(TILES_PER_HALF):
            scale_and_store(t)
        for t in range(TILES_PER_HALF, ROW_TILES):
            normalise(t)
            scale_and_store(t)
